import numpy as np
import ml_dtypes

BF16 = ml_dtypes.bfloat16


def bf(x):
    return np.asarray(x, np.float32).astype(BF16)


def f32(x):
    return np.asarray(x, np.float32)


def f64(x):
    return np.asarray(x).astype(np.float64)


def striped(idx):
    return np.tile(idx.reshape(-1, 16).T, (8, 1))


C, S, K, HEADS, DH, M, N, RUN, RUNS = 128, 512, 8, 8, 16, 256, 4096, 256, 16
TERMS = 150


def erf(a):
    a = np.asarray(a, np.float64)
    z = np.clip(a, -6.0, 6.0)
    term = z.copy()
    total = z.copy()
    for n in range(1, TERMS):
        term = term * 2.0 * z * z / (2 * n + 1)
        total = total + term
    val = 2.0 / np.sqrt(np.pi) * np.exp(-z * z) * total
    return np.where(np.abs(a) > 6.0, np.sign(a), val)


def gelu(v):
    return 0.5 * v * (1.0 + erf(v / np.sqrt(2.0)))


def setup_inputs():
    x = bf(np.random.standard_normal((C, S)))
    wkv = bf(1.5 * np.random.standard_normal((C, M)) / np.sqrt(C))
    wqr = bf(1.5 * np.random.standard_normal((C, M)) / np.sqrt(C))
    bqr = f32(0.1 * np.random.standard_normal((M, 1)))
    same_head = bf(np.kron(np.eye(HEADS), np.ones((DH, DH))))
    idx = np.concatenate([np.random.permutation(S)[:RUN] for _ in range(RUNS)])
    return {"x": x, "wkv": wkv, "wqr": wqr, "bqr": bqr, "same_head": same_head, "offs": striped(idx)}


def reference(x, wkv, wqr, bqr, same_head, offs):
    idx = offs[:16].T.reshape(-1)
    h = gelu(f64(x))
    kv = f64(wkv).T @ h[:, idx]
    qr = f64(wqr).T @ h + f64(bqr)
    key, val = kv[:C], kv[C:]
    q, res = qr[:C], qr[C:]
    prod = np.repeat(q, K, axis=1) * key
    score = f64(same_head).T @ prod / np.sqrt(DH)
    e = np.exp(score).reshape(C, S, K)
    att = (e * val.reshape(C, S, K)).sum(axis=2) / e.sum(axis=2)
    return gelu(att + res)

@@ -1,0 +1,109 @@
+import math
+
+import concourse.mybir as mybir
+
+BF16, F32, U16 = mybir.dt.bfloat16, mybir.dt.float32, mybir.dt.uint16
+ALU = mybir.AluOpType
+ACT = mybir.ActivationFunctionType
+X_AXIS = mybir.AxisListType.X
+
+C = 128
+S = 512
+K = 8
+DH = 16
+N = S * K
+PIECE = 512
+NODES = PIECE // K
+PIECES = N // PIECE
+
+FLOPS = 2 * C * (2 * C) * N + 2 * C * (2 * C) * S + 2 * C * C * N
+
+
+def tile_attnno_kernel(tc, x, wkv, wqr, bqr, same_head, offs, out):
+    nc = tc.nc
+    with (
+        tc.tile_pool(name="held", bufs=1) as held,
+        tc.tile_pool(name="work", bufs=2) as work,
+    ):
+        offsets = held.tile([C, N // 16], U16, name="offsets")
+        x_sb = held.tile([C, S], BF16, name="x_sb")
+        wkv_sb = held.tile([C, 2 * C], BF16, name="wkv_sb")
+        wqr_sb = held.tile([C, 2 * C], BF16, name="wqr_sb")
+        head_sb = held.tile([C, C], BF16, name="head_sb")
+        bias_q = held.tile([C, 1], F32, name="bias_q")
+        bias_res = held.tile([C, 1], F32, name="bias_res")
+        nc.scalar.dma_start(x_sb[:], x)
+        nc.sync.dma_start(offsets[:], offs)
+        nc.scalar.dma_start(wqr_sb[:], wqr)
+        nc.sync.dma_start(wkv_sb[:], wkv)
+        nc.scalar.dma_start(head_sb[:], same_head)
+        nc.sync.dma_start(bias_q[:], bqr[0:C, :])
+        nc.sync.dma_start(bias_res[:], bqr[C : 2 * C, :])
+
+        h = held.tile([C, S], BF16, name="h")
+        nc.scalar.activation(h[:], x_sb[:], ACT.Gelu)
+
+        q = held.tile([C, S], F32, name="q")
+        res = held.tile([C, S], F32, name="res")
+        prod = held.tile([C, S, K], BF16, name="prod")
+        val = held.tile([C, S, K], F32, name="val")
+
+        with (
+            tc.psum_pool(name="proj", bufs=1) as proj,
+            tc.psum_pool(name="picked_banks", bufs=3) as picked_banks,
+        ):
+            q_ps = proj.tile([C, S], F32, name="q_ps")
+            res_ps = proj.tile([C, S], F32, name="res_ps")
+            nc.tensor.matmul(q_ps[:], wqr_sb[:, 0:C], h[:], start=True, stop=True)
+            nc.tensor.matmul(res_ps[:], wqr_sb[:, C : 2 * C], h[:], start=True, stop=True)
+            nc.scalar.activation(q[:], q_ps[:], ACT.Identity, bias=bias_q[:])
+            nc.scalar.activation(res[:], res_ps[:], ACT.Identity, bias=bias_res[:])
+
+            for p in range(PIECES):
+                nodes = slice(p * NODES, (p + 1) * NODES)
+                picked = h[:].indirect(offsets[:, p * (PIECE // 16) : (p + 1) * (PIECE // 16)])
+                key_ps = picked_banks.tile([C, PIECE], F32, name="key_ps")
+                val_ps = picked_banks.tile([C, PIECE], F32, name="val_ps")
+                nc.tensor.matmul(key_ps[:], wkv_sb[:, 0:C], picked, start=True, stop=True)
+                nc.tensor.matmul(val_ps[:], wkv_sb[:, C : 2 * C], picked, start=True, stop=True)
+                nc.vector.tensor_tensor(
+                    prod[:, nodes, :],
+                    key_ps[:].rearrange("c (n t) -> c n t", t=K),
+                    q[:, nodes].unsqueeze(2).to_broadcast([C, NODES, K]),
+                    ALU.mult,
+                )
+                nc.scalar.copy(val[:, nodes, :], val_ps[:].rearrange("c (n t) -> c n t", t=K))
+
+        numer = held.tile([C, S], F32, name="numer")
+        denom = held.tile([C, S], F32, name="denom")
+
+        with tc.psum_pool(name="score_banks", bufs=4) as score_banks:
+            for p in range(PIECES):
+                nodes = slice(p * NODES, (p + 1) * NODES)
+                score_ps = score_banks.tile([C, PIECE], F32, name="score_ps")
+                nc.tensor.matmul(
+                    score_ps[:], head_sb[:], prod[:, nodes, :].rearrange("c n t -> c (n t)"), start=True, stop=True
+                )
+                score = score_ps[:].rearrange("c (n t) -> c n t", t=K)
+
+                top = work.tile([C, NODES], F32, name="top")
+                nc.vector.tensor_reduce(top[:], score, X_AXIS, ALU.max)
+                shifted = work.tile([C, NODES, K], F32, name="shifted")
+                nc.vector.tensor_tensor(
+                    shifted[:], score, top[:].unsqueeze(2).to_broadcast([C, NODES, K]), ALU.subtract
+                )
+                weight = work.tile([C, NODES, K], F32, name="weight")
+                nc.scalar.activation(weight[:], shifted[:], ACT.Exp, scale=1.0 / math.sqrt(DH))
+                nc.vector.tensor_reduce(denom[:, nodes], weight[:], X_AXIS, ALU.add)
+
+                weighted = work.tile([C, NODES, K], F32, name="weighted")
+                nc.vector.tensor_tensor(weighted[:], weight[:], val[:, nodes, :], ALU.mult)
+                nc.vector.tensor_reduce(numer[:, nodes], weighted[:], X_AXIS, ALU.add)
+
+        att = held.tile([C, S], F32, name="att")
+        nc.vector.reciprocal(att[:], denom[:])
+        nc.vector.tensor_tensor(att[:], att[:], numer[:], ALU.mult)
+        nc.vector.tensor_tensor(att[:], att[:], res[:], ALU.add)
+        result = held.tile([C, S], F32, name="result")
+        nc.scalar.activation(result[:], att[:], ACT.Gelu)
+        nc.sync.dma_start(out, result[:])

@@ -1,6 +1,7 @@
 import math
 
 import concourse.mybir as mybir
+from concourse.masks import make_identity
 
 BF16, F32, U16 = mybir.dt.bfloat16, mybir.dt.float32, mybir.dt.uint16
 ALU = mybir.AluOpType
@@ -15,6 +16,10 @@ N = S * K
 PIECE = 512
 NODES = PIECE // K
 PIECES = N // PIECE
+HEADS = C // DH
+BLOCK = 128
+BLOCKS = S // BLOCK
+HALVES = BLOCK // NODES
 
 FLOPS = 2 * C * (2 * C) * N + 2 * C * (2 * C) * S + 2 * C * C * N
 
@@ -40,24 +45,35 @@ def tile_attnno_kernel(tc, x, wkv, wqr, bqr, same_head, offs, out):
         nc.sync.dma_start(bias_q[:], bqr[0:C, :])
         nc.sync.dma_start(bias_res[:], bqr[C : 2 * C, :])
 
+        identity = held.tile([BLOCK, BLOCK], F32, name="identity")
+        make_identity(nc, identity[:])
+        minus_spread = held.tile([BLOCK, BLOCK, K], BF16, name="minus_spread")
+        nc.gpsimd.memset(minus_spread[:], 0.0)
+        nc.gpsimd.affine_select(
+            out=minus_spread[:].rearrange("m n t -> m (n t)"),
+            in_=minus_spread[:].rearrange("m n t -> m (n t)"),
+            pattern=[[-1, BLOCK], [0, K]],
+            compare_op=ALU.not_equal,
+            fill=-1.0,
+            base=0,
+            channel_multiplier=1,
+        )
+        head_columns = head_sb[:].rearrange("e (g d) -> e g d", d=DH)[:, :, 0]
+
         h = held.tile([C, S], BF16, name="h")
         nc.scalar.activation(h[:], x_sb[:], ACT.Gelu)
 
         q = held.tile([C, S], F32, name="q")
-        res = held.tile([C, S], F32, name="res")
         prod = held.tile([C, S, K], BF16, name="prod")
         val = held.tile([C, S, K], F32, name="val")
 
         with (
-            tc.psum_pool(name="proj", bufs=1) as proj,
+            tc.psum_pool(name="q_bank", bufs=1) as q_bank,
             tc.psum_pool(name="picked_banks", bufs=3) as picked_banks,
         ):
-            q_ps = proj.tile([C, S], F32, name="q_ps")
-            res_ps = proj.tile([C, S], F32, name="res_ps")
+            q_ps = q_bank.tile([C, S], F32, name="q_ps")
             nc.tensor.matmul(q_ps[:], wqr_sb[:, 0:C], h[:], start=True, stop=True)
-            nc.tensor.matmul(res_ps[:], wqr_sb[:, C : 2 * C], h[:], start=True, stop=True)
             nc.scalar.activation(q[:], q_ps[:], ACT.Identity, bias=bias_q[:])
-            nc.scalar.activation(res[:], res_ps[:], ACT.Identity, bias=bias_res[:])
 
             for p in range(PIECES):
                 nodes = slice(p * NODES, (p + 1) * NODES)
@@ -75,35 +91,68 @@ def tile_attnno_kernel(tc, x, wkv, wqr, bqr, same_head, offs, out):
                 nc.scalar.copy(val[:, nodes, :], val_ps[:].rearrange("c (n t) -> c n t", t=K))
 
         numer = held.tile([C, S], F32, name="numer")
-        denom = held.tile([C, S], F32, name="denom")
-
-        with tc.psum_pool(name="score_banks", bufs=4) as score_banks:
-            for p in range(PIECES):
-                nodes = slice(p * NODES, (p + 1) * NODES)
-                score_ps = score_banks.tile([C, PIECE], F32, name="score_ps")
-                nc.tensor.matmul(
-                    score_ps[:], head_sb[:], prod[:, nodes, :].rearrange("c n t -> c (n t)"), start=True, stop=True
-                )
-                score = score_ps[:].rearrange("c (n t) -> c n t", t=K)
-
-                top = work.tile([C, NODES], F32, name="top")
-                nc.vector.tensor_reduce(top[:], score, X_AXIS, ALU.max)
-                shifted = work.tile([C, NODES, K], F32, name="shifted")
-                nc.vector.tensor_tensor(
-                    shifted[:], score, top[:].unsqueeze(2).to_broadcast([C, NODES, K]), ALU.subtract
-                )
-                weight = work.tile([C, NODES, K], F32, name="weight")
-                nc.scalar.activation(weight[:], shifted[:], ACT.Exp, scale=1.0 / math.sqrt(DH))
-                nc.vector.tensor_reduce(denom[:, nodes], weight[:], X_AXIS, ALU.add)
-
-                weighted = work.tile([C, NODES, K], F32, name="weighted")
-                nc.vector.tensor_tensor(weighted[:], weight[:], val[:, nodes, :], ALU.mult)
-                nc.vector.tensor_reduce(numer[:, nodes], weighted[:], X_AXIS, ALU.add)
-
         att = held.tile([C, S], F32, name="att")
-        nc.vector.reciprocal(att[:], denom[:])
-        nc.vector.tensor_tensor(att[:], att[:], numer[:], ALU.mult)
-        nc.vector.tensor_tensor(att[:], att[:], res[:], ALU.add)
-        result = held.tile([C, S], F32, name="result")
-        nc.scalar.activation(result[:], att[:], ACT.Gelu)
-        nc.sync.dma_start(out, result[:])
+
+        with (
+            tc.psum_pool(name="res_bank", bufs=1) as res_bank,
+            tc.psum_pool(name="by_node_banks", bufs=2) as by_node_banks,
+            tc.psum_pool(name="score_banks", bufs=3) as score_banks,
+            tc.psum_pool(name="rden_banks", bufs=2) as rden_banks,
+        ):
+            res_ps = res_bank.tile([C, S], F32, name="res_ps")
+            nc.tensor.matmul(res_ps[:], wqr_sb[:, C : 2 * C], h[:], start=True, stop=True)
+
+            for b in range(BLOCKS):
+                block = slice(b * BLOCK, (b + 1) * BLOCK)
+
+                by_node_ps = by_node_banks.tile([BLOCK, K, HEADS], F32, name="by_node_ps")
+                for t in range(K):
+                    nc.tensor.matmul(by_node_ps[:, t, :], prod[:, block, t], head_columns, start=True, stop=True)
+
+                top = work.tile([BLOCK, HEADS], F32, name="top")
+                nc.vector.tensor_reduce(top[:], by_node_ps[:].rearrange("n t g -> n g t"), X_AXIS, ALU.max)
+                top_rep = work.tile([BLOCK, HEADS, DH], BF16, name="top_rep")
+                nc.vector.tensor_copy(top_rep[:], top[:].unsqueeze(2).to_broadcast([BLOCK, HEADS, DH]))
+
+                for half in range(HALVES):
+                    first = b * BLOCK + half * NODES
+                    nodes = slice(first, first + NODES)
+                    score_ps = score_banks.tile([C, PIECE], F32, name="score_ps")
+                    nc.tensor.matmul(
+                        score_ps[:], head_sb[:], prod[:, nodes, :].rearrange("c n t -> c (n t)"),
+                        start=True, stop=False,
+                    )
+                    nc.tensor.matmul(
+                        score_ps[:],
+                        top_rep[:].rearrange("n g d -> n (g d)"),
+                        minus_spread[:, half * NODES : (half + 1) * NODES, :].rearrange("m n t -> m (n t)"),
+                        start=False, stop=True,
+                    )
+                    weight = work.tile([C, NODES, K], F32, name="weight")
+                    nc.scalar.activation(
+                        weight[:].rearrange("c n t -> c (n t)"), score_ps[:], ACT.Exp, scale=1.0 / math.sqrt(DH)
+                    )
+                    weighted = work.tile([C, NODES, K], F32, name="weighted")
+                    nc.vector.tensor_tensor(weighted[:], weight[:], val[:, nodes, :], ALU.mult)
+                    nc.vector.tensor_reduce(numer[:, nodes], weighted[:], X_AXIS, ALU.add)
+
+                shifted = work.tile([BLOCK, K, HEADS], F32, name="shifted")
+                nc.vector.tensor_tensor(
+                    shifted[:], by_node_ps[:], top_rep[:, :, 0].unsqueeze(1).to_broadcast([BLOCK, K, HEADS]),
+                    ALU.subtract,
+                )
+                nc.scalar.activation(shifted[:], shifted[:], ACT.Exp, scale=1.0 / math.sqrt(DH))
+                rden = work.tile([BLOCK, HEADS], F32, name="rden")
+                nc.vector.tensor_reduce(rden[:], shifted[:].rearrange("n t g -> n g t"), X_AXIS, ALU.add)
+                nc.vector.reciprocal(rden[:], rden[:])
+                rden_rep = work.tile([BLOCK, HEADS, DH], F32, name="rden_rep")
+                nc.vector.tensor_copy(rden_rep[:], rden[:].unsqueeze(2).to_broadcast([BLOCK, HEADS, DH]))
+                rden_ps = rden_banks.tile([C, BLOCK], F32, name="rden_ps")
+                nc.tensor.transpose(rden_ps[:], rden_rep[:].rearrange("n g d -> n (g d)"), identity[:])
+
+                nc.vector.tensor_tensor(att[:, block], numer[:, block], rden_ps[:], ALU.mult)
+                nc.vector.tensor_tensor(att[:, block], att[:, block], res_ps[:, block], ALU.add)
+
+            result = held.tile([C, S], F32, name="result")
+            nc.scalar.activation(result[:], att[:], ACT.Gelu, bias=bias_res[:])
+            nc.sync.dma_start(out, result[:])

@@ -20,6 +20,7 @@ HEADS = C // DH
 BLOCK = 128
 BLOCKS = S // BLOCK
 HALVES = BLOCK // NODES
+WARM_UP = 3
 
 FLOPS = 2 * C * (2 * C) * N + 2 * C * (2 * C) * S + 2 * C * C * N
 
@@ -38,12 +39,19 @@ def tile_attnno_kernel(tc, x, wkv, wqr, bqr, same_head, offs, out):
         bias_q = held.tile([C, 1], F32, name="bias_q")
         bias_res = held.tile([C, 1], F32, name="bias_res")
         nc.scalar.dma_start(x_sb[:], x)
+        nc.sync.dma_start(wqr_sb[:], wqr)
         nc.sync.dma_start(offsets[:], offs)
-        nc.scalar.dma_start(wqr_sb[:], wqr)
         nc.sync.dma_start(wkv_sb[:], wkv)
-        nc.scalar.dma_start(head_sb[:], same_head)
         nc.sync.dma_start(bias_q[:], bqr[0:C, :])
         nc.sync.dma_start(bias_res[:], bqr[C : 2 * C, :])
+        nc.sync.dma_start(head_sb[:], same_head)
+
+        zeros = held.tile([C, S], BF16, name="zeros")
+        nc.gpsimd.memset(zeros[:], 0.0)
+        with tc.psum_pool(name="warm_bank", bufs=1) as warm_bank:
+            warm_ps = warm_bank.tile([C, S], F32, name="warm_ps")
+            for i in range(WARM_UP):
+                nc.tensor.matmul(warm_ps[:], zeros[:, 0:C], zeros[:], start=True, stop=True)
 
         identity = held.tile([BLOCK, BLOCK], F32, name="identity")
         make_identity(nc, identity[:])
@@ -64,16 +72,20 @@ def tile_attnno_kernel(tc, x, wkv, wqr, bqr, same_head, offs, out):
         nc.scalar.activation(h[:], x_sb[:], ACT.Gelu)
 
         q = held.tile([C, S], F32, name="q")
+        res = held.tile([C, S], F32, name="res")
         prod = held.tile([C, S, K], BF16, name="prod")
         val = held.tile([C, S, K], F32, name="val")
 
         with (
-            tc.psum_pool(name="q_bank", bufs=1) as q_bank,
+            tc.psum_pool(name="plain_banks", bufs=1) as plain_banks,
             tc.psum_pool(name="picked_banks", bufs=3) as picked_banks,
         ):
-            q_ps = q_bank.tile([C, S], F32, name="q_ps")
+            q_ps = plain_banks.tile([C, S], F32, name="q_ps")
+            res_ps = plain_banks.tile([C, S], F32, name="res_ps")
             nc.tensor.matmul(q_ps[:], wqr_sb[:, 0:C], h[:], start=True, stop=True)
+            nc.tensor.matmul(res_ps[:], wqr_sb[:, C : 2 * C], h[:], start=True, stop=True)
             nc.scalar.activation(q[:], q_ps[:], ACT.Identity, bias=bias_q[:])
+            nc.scalar.activation(res[:], res_ps[:], ACT.Identity, bias=bias_res[:])
 
             for p in range(PIECES):
                 nodes = slice(p * NODES, (p + 1) * NODES)
@@ -89,18 +101,22 @@ def tile_attnno_kernel(tc, x, wkv, wqr, bqr, same_head, offs, out):
                     ALU.mult,
                 )
                 nc.scalar.copy(val[:, nodes, :], val_ps[:].rearrange("c (n t) -> c n t", t=K))
+                nc.gpsimd.tensor_tensor(
+                    val[:, nodes, :], val[:, nodes, :], res[:, nodes].unsqueeze(2).to_broadcast([C, NODES, K]), ALU.add
+                )
 
         numer = held.tile([C, S], F32, name="numer")
         att = held.tile([C, S], F32, name="att")
+        result = held.tile([C, S], F32, name="result")
 
         with (
-            tc.psum_pool(name="res_bank", bufs=1) as res_bank,
+            tc.tile_pool(name="weights", bufs=PIECES) as weights,
+            tc.psum_pool(name="rden_bank", bufs=1) as rden_bank,
             tc.psum_pool(name="by_node_banks", bufs=2) as by_node_banks,
-            tc.psum_pool(name="score_banks", bufs=3) as score_banks,
-            tc.psum_pool(name="rden_banks", bufs=2) as rden_banks,
+            tc.psum_pool(name="score_banks", bufs=4) as score_banks,
         ):
-            res_ps = res_bank.tile([C, S], F32, name="res_ps")
-            nc.tensor.matmul(res_ps[:], wqr_sb[:, C : 2 * C], h[:], start=True, stop=True)
+            rden_ps = rden_bank.tile([C, S], F32, name="rden_ps")
+            weight_of = []
 
             for b in range(BLOCKS):
                 block = slice(b * BLOCK, (b + 1) * BLOCK)
@@ -116,10 +132,9 @@ def tile_attnno_kernel(tc, x, wkv, wqr, bqr, same_head, offs, out):
 
                 for half in range(HALVES):
                     first = b * BLOCK + half * NODES
-                    nodes = slice(first, first + NODES)
                     score_ps = score_banks.tile([C, PIECE], F32, name="score_ps")
                     nc.tensor.matmul(
-                        score_ps[:], head_sb[:], prod[:, nodes, :].rearrange("c n t -> c (n t)"),
+                        score_ps[:], head_sb[:], prod[:, first : first + NODES, :].rearrange("c n t -> c (n t)"),
                         start=True, stop=False,
                     )
                     nc.tensor.matmul(
@@ -128,13 +143,11 @@ def tile_attnno_kernel(tc, x, wkv, wqr, bqr, same_head, offs, out):
                         minus_spread[:, half * NODES : (half + 1) * NODES, :].rearrange("m n t -> m (n t)"),
                         start=False, stop=True,
                     )
-                    weight = work.tile([C, NODES, K], F32, name="weight")
+                    weight = weights.tile([C, NODES, K], F32, name="weight")
                     nc.scalar.activation(
                         weight[:].rearrange("c n t -> c (n t)"), score_ps[:], ACT.Exp, scale=1.0 / math.sqrt(DH)
                     )
-                    weighted = work.tile([C, NODES, K], F32, name="weighted")
-                    nc.vector.tensor_tensor(weighted[:], weight[:], val[:, nodes, :], ALU.mult)
-                    nc.vector.tensor_reduce(numer[:, nodes], weighted[:], X_AXIS, ALU.add)
+                    weight_of.append(weight)
 
                 shifted = work.tile([BLOCK, K, HEADS], F32, name="shifted")
                 nc.vector.tensor_tensor(
@@ -142,17 +155,29 @@ def tile_attnno_kernel(tc, x, wkv, wqr, bqr, same_head, offs, out):
                     ALU.subtract,
                 )
                 nc.scalar.activation(shifted[:], shifted[:], ACT.Exp, scale=1.0 / math.sqrt(DH))
-                rden = work.tile([BLOCK, HEADS], F32, name="rden")
-                nc.vector.tensor_reduce(rden[:], shifted[:].rearrange("n t g -> n g t"), X_AXIS, ALU.add)
-                nc.vector.reciprocal(rden[:], rden[:])
+                rden_small = work.tile([BLOCK, HEADS], F32, name="rden_small")
+                nc.vector.tensor_reduce(rden_small[:], shifted[:].rearrange("n t g -> n g t"), X_AXIS, ALU.add)
+                nc.vector.reciprocal(rden_small[:], rden_small[:])
                 rden_rep = work.tile([BLOCK, HEADS, DH], F32, name="rden_rep")
-                nc.vector.tensor_copy(rden_rep[:], rden[:].unsqueeze(2).to_broadcast([BLOCK, HEADS, DH]))
-                rden_ps = rden_banks.tile([C, BLOCK], F32, name="rden_ps")
-                nc.tensor.transpose(rden_ps[:], rden_rep[:].rearrange("n g d -> n (g d)"), identity[:])
+                nc.scalar.copy(rden_rep[:], rden_small[:].unsqueeze(2).to_broadcast([BLOCK, HEADS, DH]))
+                nc.tensor.transpose(rden_ps[:, block], rden_rep[:].rearrange("n g d -> n (g d)"), identity[:])
 
-                nc.vector.tensor_tensor(att[:, block], numer[:, block], rden_ps[:], ALU.mult)
-                nc.vector.tensor_tensor(att[:, block], att[:, block], res_ps[:, block], ALU.add)
-
-            result = held.tile([C, S], F32, name="result")
-            nc.scalar.activation(result[:], att[:], ACT.Gelu, bias=bias_res[:])
-            nc.sync.dma_start(out, result[:])
+            for first_piece, end_piece in ((0, PIECES - HALVES), (PIECES - HALVES, PIECES)):
+                columns = slice(first_piece * NODES, end_piece * NODES)
+                for p in range(first_piece, end_piece):
+                    nodes = slice(p * NODES, (p + 1) * NODES)
+                    if p % HALVES == 1 and p < PIECES // 2:
+                        halved = work.tile([C, NODES, K], F32, name="halved")
+                        nc.gpsimd.tensor_tensor(halved[:], weight_of[p][:], val[:, nodes, :], ALU.mult)
+                        for width in (4, 2):
+                            nc.gpsimd.tensor_tensor(
+                                halved[:, :, 0:width], halved[:, :, 0:width], halved[:, :, width : 2 * width], ALU.add
+                            )
+                        nc.gpsimd.tensor_tensor(numer[:, nodes], halved[:, :, 0], halved[:, :, 1], ALU.add)
+                    else:
+                        weighted = work.tile([C, NODES, K], F32, name="weighted")
+                        nc.vector.tensor_tensor(weighted[:], weight_of[p][:], val[:, nodes, :], ALU.mult)
+                        nc.vector.tensor_reduce(numer[:, nodes], weighted[:], X_AXIS, ALU.add)
+                nc.vector.tensor_tensor(att[:, columns], numer[:, columns], rden_ps[:, columns], ALU.mult)
+                nc.scalar.activation(result[:, columns], att[:, columns], ACT.Gelu)
+                nc.sync.dma_start(out[:, columns], result[:, columns])

@@ -166,18 +166,9 @@ def tile_attnno_kernel(tc, x, wkv, wqr, bqr, same_head, offs, out):
                 columns = slice(first_piece * NODES, end_piece * NODES)
                 for p in range(first_piece, end_piece):
                     nodes = slice(p * NODES, (p + 1) * NODES)
-                    if p % HALVES == 1 and p < PIECES // 2:
-                        halved = work.tile([C, NODES, K], F32, name="halved")
-                        nc.gpsimd.tensor_tensor(halved[:], weight_of[p][:], val[:, nodes, :], ALU.mult)
-                        for width in (4, 2):
-                            nc.gpsimd.tensor_tensor(
-                                halved[:, :, 0:width], halved[:, :, 0:width], halved[:, :, width : 2 * width], ALU.add
-                            )
-                        nc.gpsimd.tensor_tensor(numer[:, nodes], halved[:, :, 0], halved[:, :, 1], ALU.add)
-                    else:
-                        weighted = work.tile([C, NODES, K], F32, name="weighted")
-                        nc.vector.tensor_tensor(weighted[:], weight_of[p][:], val[:, nodes, :], ALU.mult)
-                        nc.vector.tensor_reduce(numer[:, nodes], weighted[:], X_AXIS, ALU.add)
+                    weighted = work.tile([C, NODES, K], F32, name="weighted")
+                    nc.vector.tensor_tensor(weighted[:], weight_of[p][:], val[:, nodes, :], ALU.mult)
+                    nc.vector.tensor_reduce(numer[:, nodes], weighted[:], X_AXIS, ALU.add)
                 nc.vector.tensor_tensor(att[:, columns], numer[:, columns], rden_ps[:, columns], ALU.mult)
                 nc.scalar.activation(result[:, columns], att[:, columns], ACT.Gelu)
                 nc.sync.dma_start(out[:, columns], result[:, columns])

@@ -108,29 +108,34 @@ def tile_attnno_kernel(tc, x, wkv, wqr, bqr, same_head, offs, out):
         numer = held.tile([C, S], F32, name="numer")
         att = held.tile([C, S], F32, name="att")
         result = held.tile([C, S], F32, name="result")
+        top_rep = held.tile([BLOCK, BLOCKS, HEADS, DH], BF16, name="top_rep")
+        shifted = held.tile([BLOCK, BLOCKS, K, HEADS], F32, name="shifted")
+        rden_small = held.tile([BLOCK, BLOCKS, HEADS], F32, name="rden_small")
+        rden_rep = held.tile([BLOCK, BLOCKS, HEADS, DH], F32, name="rden_rep")
 
         with (
-            tc.tile_pool(name="weights", bufs=PIECES) as weights,
-            tc.psum_pool(name="rden_bank", bufs=1) as rden_bank,
-            tc.psum_pool(name="by_node_banks", bufs=2) as by_node_banks,
+            tc.tile_pool(name="weights", bufs=BLOCKS) as weights,
+            tc.psum_pool(name="whole_banks", bufs=1) as whole_banks,
             tc.psum_pool(name="score_banks", bufs=4) as score_banks,
         ):
-            rden_ps = rden_bank.tile([C, S], F32, name="rden_ps")
+            by_node_ps = whole_banks.tile([BLOCK, BLOCKS, K, HEADS], F32, name="by_node_ps")
+            rden_ps = whole_banks.tile([C, S], F32, name="rden_ps")
             weight_of = []
 
             for b in range(BLOCKS):
                 block = slice(b * BLOCK, (b + 1) * BLOCK)
 
-                by_node_ps = by_node_banks.tile([BLOCK, K, HEADS], F32, name="by_node_ps")
                 for t in range(K):
-                    nc.tensor.matmul(by_node_ps[:, t, :], prod[:, block, t], head_columns, start=True, stop=True)
+                    nc.tensor.matmul(by_node_ps[:, b, t, :], prod[:, block, t], head_columns, start=True, stop=True)
 
                 top = work.tile([BLOCK, HEADS], F32, name="top")
-                nc.vector.tensor_reduce(top[:], by_node_ps[:].rearrange("n t g -> n g t"), X_AXIS, ALU.max)
-                top_rep = work.tile([BLOCK, HEADS, DH], BF16, name="top_rep")
-                nc.vector.tensor_copy(top_rep[:], top[:].unsqueeze(2).to_broadcast([BLOCK, HEADS, DH]))
+                nc.vector.tensor_reduce(top[:], by_node_ps[:, b].rearrange("n t g -> n g t"), X_AXIS, ALU.max)
+                nc.vector.tensor_copy(top_rep[:, b], top[:].unsqueeze(2).to_broadcast([BLOCK, HEADS, DH]))
 
+                weight = weights.tile([C, BLOCK, K], F32, name="weight")
+                weight_of.append(weight)
                 for half in range(HALVES):
+                    in_block = slice(half * NODES, (half + 1) * NODES)
                     first = b * BLOCK + half * NODES
                     score_ps = score_banks.tile([C, PIECE], F32, name="score_ps")
                     nc.tensor.matmul(
@@ -139,36 +144,40 @@ def tile_attnno_kernel(tc, x, wkv, wqr, bqr, same_head, offs, out):
                     )
                     nc.tensor.matmul(
                         score_ps[:],
-                        top_rep[:].rearrange("n g d -> n (g d)"),
-                        minus_spread[:, half * NODES : (half + 1) * NODES, :].rearrange("m n t -> m (n t)"),
+                        top_rep[:, b].rearrange("n g d -> n (g d)"),
+                        minus_spread[:, in_block, :].rearrange("m n t -> m (n t)"),
                         start=False, stop=True,
                     )
-                    weight = weights.tile([C, NODES, K], F32, name="weight")
                     nc.scalar.activation(
-                        weight[:].rearrange("c n t -> c (n t)"), score_ps[:], ACT.Exp, scale=1.0 / math.sqrt(DH)
+                        weight[:, in_block, :].rearrange("c n t -> c (n t)"), score_ps[:], ACT.Exp,
+                        scale=1.0 / math.sqrt(DH),
                     )
-                    weight_of.append(weight)
 
-                shifted = work.tile([BLOCK, K, HEADS], F32, name="shifted")
-                nc.vector.tensor_tensor(
-                    shifted[:], by_node_ps[:], top_rep[:, :, 0].unsqueeze(1).to_broadcast([BLOCK, K, HEADS]),
-                    ALU.subtract,
+            nc.vector.tensor_tensor(
+                shifted[:], by_node_ps[:], top_rep[:, :, :, 0].unsqueeze(2).to_broadcast([BLOCK, BLOCKS, K, HEADS]),
+                ALU.subtract,
+            )
+            nc.scalar.activation(shifted[:], shifted[:], ACT.Exp, scale=1.0 / math.sqrt(DH))
+            nc.vector.tensor_reduce(rden_small[:], shifted[:].rearrange("n b t g -> n b g t"), X_AXIS, ALU.add)
+            nc.vector.reciprocal(rden_small[:], rden_small[:])
+            nc.scalar.copy(rden_rep[:], rden_small[:].unsqueeze(3).to_broadcast([BLOCK, BLOCKS, HEADS, DH]))
+            for b in range(BLOCKS):
+                nc.tensor.transpose(
+                    rden_ps[:, b * BLOCK : (b + 1) * BLOCK], rden_rep[:, b].rearrange("n g d -> n (g d)"), identity[:]
                 )
-                nc.scalar.activation(shifted[:], shifted[:], ACT.Exp, scale=1.0 / math.sqrt(DH))
-                rden_small = work.tile([BLOCK, HEADS], F32, name="rden_small")
-                nc.vector.tensor_reduce(rden_small[:], shifted[:].rearrange("n t g -> n g t"), X_AXIS, ALU.add)
-                nc.vector.reciprocal(rden_small[:], rden_small[:])
-                rden_rep = work.tile([BLOCK, HEADS, DH], F32, name="rden_rep")
-                nc.scalar.copy(rden_rep[:], rden_small[:].unsqueeze(2).to_broadcast([BLOCK, HEADS, DH]))
-                nc.tensor.transpose(rden_ps[:, block], rden_rep[:].rearrange("n g d -> n (g d)"), identity[:])
 
-            for first_piece, end_piece in ((0, PIECES - HALVES), (PIECES - HALVES, PIECES)):
-                columns = slice(first_piece * NODES, end_piece * NODES)
-                for p in range(first_piece, end_piece):
-                    nodes = slice(p * NODES, (p + 1) * NODES)
-                    weighted = work.tile([C, NODES, K], F32, name="weighted")
-                    nc.vector.tensor_tensor(weighted[:], weight_of[p][:], val[:, nodes, :], ALU.mult)
-                    nc.vector.tensor_reduce(numer[:, nodes], weighted[:], X_AXIS, ALU.add)
+            weighted_of = []
+            for b in range(BLOCKS + 1):
+                if b < BLOCKS:
+                    weighted = work.tile([C, BLOCK, K], F32, name="weighted")
+                    nc.vector.tensor_tensor(
+                        weighted[:], weight_of[b][:], val[:, b * BLOCK : (b + 1) * BLOCK, :], ALU.mult
+                    )
+                    weighted_of.append(weighted)
+                if b > 0:
+                    nc.vector.tensor_reduce(numer[:, (b - 1) * BLOCK : b * BLOCK], weighted_of[b - 1][:], X_AXIS, ALU.add)
+
+            for columns in (slice(0, S - BLOCK), slice(S - BLOCK, S)):
                 nc.vector.tensor_tensor(att[:, columns], numer[:, columns], rden_ps[:, columns], ALU.mult)
                 nc.scalar.activation(result[:, columns], att[:, columns], ACT.Gelu)
                 nc.sync.dma_start(out[:, columns], result[:, columns])

@@ -101,41 +101,33 @@ def tile_attnno_kernel(tc, x, wkv, wqr, bqr, same_head, offs, out):
                     ALU.mult,
                 )
                 nc.scalar.copy(val[:, nodes, :], val_ps[:].rearrange("c (n t) -> c n t", t=K))
-                nc.gpsimd.tensor_tensor(
-                    val[:, nodes, :], val[:, nodes, :], res[:, nodes].unsqueeze(2).to_broadcast([C, NODES, K]), ALU.add
-                )
 
         numer = held.tile([C, S], F32, name="numer")
         att = held.tile([C, S], F32, name="att")
         result = held.tile([C, S], F32, name="result")
-        top_rep = held.tile([BLOCK, BLOCKS, HEADS, DH], BF16, name="top_rep")
-        shifted = held.tile([BLOCK, BLOCKS, K, HEADS], F32, name="shifted")
-        rden_small = held.tile([BLOCK, BLOCKS, HEADS], F32, name="rden_small")
-        rden_rep = held.tile([BLOCK, BLOCKS, HEADS, DH], F32, name="rden_rep")
 
         with (
-            tc.tile_pool(name="weights", bufs=BLOCKS) as weights,
-            tc.psum_pool(name="whole_banks", bufs=1) as whole_banks,
+            tc.tile_pool(name="weights", bufs=PIECES) as weights,
+            tc.psum_pool(name="rden_bank", bufs=1) as rden_bank,
+            tc.psum_pool(name="by_node_banks", bufs=2) as by_node_banks,
             tc.psum_pool(name="score_banks", bufs=4) as score_banks,
         ):
-            by_node_ps = whole_banks.tile([BLOCK, BLOCKS, K, HEADS], F32, name="by_node_ps")
-            rden_ps = whole_banks.tile([C, S], F32, name="rden_ps")
+            rden_ps = rden_bank.tile([C, S], F32, name="rden_ps")
             weight_of = []
 
             for b in range(BLOCKS):
                 block = slice(b * BLOCK, (b + 1) * BLOCK)
 
+                by_node_ps = by_node_banks.tile([BLOCK, K, HEADS], F32, name="by_node_ps")
                 for t in range(K):
-                    nc.tensor.matmul(by_node_ps[:, b, t, :], prod[:, block, t], head_columns, start=True, stop=True)
+                    nc.tensor.matmul(by_node_ps[:, t, :], prod[:, block, t], head_columns, start=True, stop=True)
 
                 top = work.tile([BLOCK, HEADS], F32, name="top")
-                nc.vector.tensor_reduce(top[:], by_node_ps[:, b].rearrange("n t g -> n g t"), X_AXIS, ALU.max)
-                nc.vector.tensor_copy(top_rep[:, b], top[:].unsqueeze(2).to_broadcast([BLOCK, HEADS, DH]))
+                nc.vector.tensor_reduce(top[:], by_node_ps[:].rearrange("n t g -> n g t"), X_AXIS, ALU.max)
+                top_rep = work.tile([BLOCK, HEADS, DH], BF16, name="top_rep")
+                nc.vector.tensor_copy(top_rep[:], top[:].unsqueeze(2).to_broadcast([BLOCK, HEADS, DH]))
 
-                weight = weights.tile([C, BLOCK, K], F32, name="weight")
-                weight_of.append(weight)
                 for half in range(HALVES):
-                    in_block = slice(half * NODES, (half + 1) * NODES)
                     first = b * BLOCK + half * NODES
                     score_ps = score_banks.tile([C, PIECE], F32, name="score_ps")
                     nc.tensor.matmul(
@@ -144,40 +136,37 @@ def tile_attnno_kernel(tc, x, wkv, wqr, bqr, same_head, offs, out):
                     )
                     nc.tensor.matmul(
                         score_ps[:],
-                        top_rep[:, b].rearrange("n g d -> n (g d)"),
-                        minus_spread[:, in_block, :].rearrange("m n t -> m (n t)"),
+                        top_rep[:].rearrange("n g d -> n (g d)"),
+                        minus_spread[:, half * NODES : (half + 1) * NODES, :].rearrange("m n t -> m (n t)"),
                         start=False, stop=True,
                     )
+                    weight = weights.tile([C, NODES, K], F32, name="weight")
                     nc.scalar.activation(
-                        weight[:, in_block, :].rearrange("c n t -> c (n t)"), score_ps[:], ACT.Exp,
-                        scale=1.0 / math.sqrt(DH),
+                        weight[:].rearrange("c n t -> c (n t)"), score_ps[:], ACT.Exp, scale=1.0 / math.sqrt(DH)
                     )
+                    weight_of.append(weight)
 
-            nc.vector.tensor_tensor(
-                shifted[:], by_node_ps[:], top_rep[:, :, :, 0].unsqueeze(2).to_broadcast([BLOCK, BLOCKS, K, HEADS]),
-                ALU.subtract,
-            )
-            nc.scalar.activation(shifted[:], shifted[:], ACT.Exp, scale=1.0 / math.sqrt(DH))
-            nc.vector.tensor_reduce(rden_small[:], shifted[:].rearrange("n b t g -> n b g t"), X_AXIS, ALU.add)
-            nc.vector.reciprocal(rden_small[:], rden_small[:])
-            nc.scalar.copy(rden_rep[:], rden_small[:].unsqueeze(3).to_broadcast([BLOCK, BLOCKS, HEADS, DH]))
-            for b in range(BLOCKS):
-                nc.tensor.transpose(
-                    rden_ps[:, b * BLOCK : (b + 1) * BLOCK], rden_rep[:, b].rearrange("n g d -> n (g d)"), identity[:]
+                shifted = work.tile([BLOCK, K, HEADS], F32, name="shifted")
+                nc.vector.tensor_tensor(
+                    shifted[:], by_node_ps[:], top_rep[:, :, 0].unsqueeze(1).to_broadcast([BLOCK, K, HEADS]),
+                    ALU.subtract,
                 )
+                nc.scalar.activation(shifted[:], shifted[:], ACT.Exp, scale=1.0 / math.sqrt(DH))
+                rden_small = work.tile([BLOCK, HEADS], F32, name="rden_small")
+                nc.vector.tensor_reduce(rden_small[:], shifted[:].rearrange("n t g -> n g t"), X_AXIS, ALU.add)
+                nc.vector.reciprocal(rden_small[:], rden_small[:])
+                rden_rep = work.tile([BLOCK, HEADS, DH], F32, name="rden_rep")
+                nc.scalar.copy(rden_rep[:], rden_small[:].unsqueeze(2).to_broadcast([BLOCK, HEADS, DH]))
+                nc.tensor.transpose(rden_ps[:, block], rden_rep[:].rearrange("n g d -> n (g d)"), identity[:])
 
-            weighted_of = []
-            for b in range(BLOCKS + 1):
-                if b < BLOCKS:
-                    weighted = work.tile([C, BLOCK, K], F32, name="weighted")
-                    nc.vector.tensor_tensor(
-                        weighted[:], weight_of[b][:], val[:, b * BLOCK : (b + 1) * BLOCK, :], ALU.mult
-                    )
-                    weighted_of.append(weighted)
-                if b > 0:
-                    nc.vector.tensor_reduce(numer[:, (b - 1) * BLOCK : b * BLOCK], weighted_of[b - 1][:], X_AXIS, ALU.add)
-
-            for columns in (slice(0, S - BLOCK), slice(S - BLOCK, S)):
+            for first_piece, end_piece in ((0, PIECES - HALVES), (PIECES - HALVES, PIECES)):
+                columns = slice(first_piece * NODES, end_piece * NODES)
+                for p in range(first_piece, end_piece):
+                    nodes = slice(p * NODES, (p + 1) * NODES)
+                    weighted = work.tile([C, NODES, K], F32, name="weighted")
+                    nc.vector.tensor_tensor(weighted[:], weight_of[p][:], val[:, nodes, :], ALU.mult)
+                    nc.vector.tensor_reduce(numer[:, nodes], weighted[:], X_AXIS, ALU.add)
                 nc.vector.tensor_tensor(att[:, columns], numer[:, columns], rden_ps[:, columns], ALU.mult)
+                nc.vector.tensor_tensor(att[:, columns], att[:, columns], res[:, columns], ALU.add)
                 nc.scalar.activation(result[:, columns], att[:, columns], ACT.Gelu)
                 nc.sync.dma_start(out[:, columns], result[:, columns])

@@ -107,12 +107,14 @@ def tile_attnno_kernel(tc, x, wkv, wqr, bqr, same_head, offs, out):
         result = held.tile([C, S], F32, name="result")
 
         with (
+            tc.tile_pool(name="shifts", bufs=BLOCKS) as shifts,
             tc.tile_pool(name="weights", bufs=PIECES) as weights,
             tc.psum_pool(name="rden_bank", bufs=1) as rden_bank,
-            tc.psum_pool(name="by_node_banks", bufs=2) as by_node_banks,
-            tc.psum_pool(name="score_banks", bufs=4) as score_banks,
+            tc.psum_pool(name="by_node_banks", bufs=BLOCKS) as by_node_banks,
+            tc.psum_pool(name="score_banks", bufs=3) as score_banks,
         ):
             rden_ps = rden_bank.tile([C, S], F32, name="rden_ps")
+            top_rep_of = []
             weight_of = []
 
             for b in range(BLOCKS):
@@ -124,27 +126,9 @@ def tile_attnno_kernel(tc, x, wkv, wqr, bqr, same_head, offs, out):
 
                 top = work.tile([BLOCK, HEADS], F32, name="top")
                 nc.vector.tensor_reduce(top[:], by_node_ps[:].rearrange("n t g -> n g t"), X_AXIS, ALU.max)
-                top_rep = work.tile([BLOCK, HEADS, DH], BF16, name="top_rep")
+                top_rep = shifts.tile([BLOCK, HEADS, DH], BF16, name="top_rep")
                 nc.vector.tensor_copy(top_rep[:], top[:].unsqueeze(2).to_broadcast([BLOCK, HEADS, DH]))
-
-                for half in range(HALVES):
-                    first = b * BLOCK + half * NODES
-                    score_ps = score_banks.tile([C, PIECE], F32, name="score_ps")
-                    nc.tensor.matmul(
-                        score_ps[:], head_sb[:], prod[:, first : first + NODES, :].rearrange("c n t -> c (n t)"),
-                        start=True, stop=False,
-                    )
-                    nc.tensor.matmul(
-                        score_ps[:],
-                        top_rep[:].rearrange("n g d -> n (g d)"),
-                        minus_spread[:, half * NODES : (half + 1) * NODES, :].rearrange("m n t -> m (n t)"),
-                        start=False, stop=True,
-                    )
-                    weight = weights.tile([C, NODES, K], F32, name="weight")
-                    nc.scalar.activation(
-                        weight[:].rearrange("c n t -> c (n t)"), score_ps[:], ACT.Exp, scale=1.0 / math.sqrt(DH)
-                    )
-                    weight_of.append(weight)
+                top_rep_of.append(top_rep)
 
                 shifted = work.tile([BLOCK, K, HEADS], F32, name="shifted")
                 nc.vector.tensor_tensor(
@@ -158,6 +142,25 @@ def tile_attnno_kernel(tc, x, wkv, wqr, bqr, same_head, offs, out):
                 rden_rep = work.tile([BLOCK, HEADS, DH], F32, name="rden_rep")
                 nc.scalar.copy(rden_rep[:], rden_small[:].unsqueeze(2).to_broadcast([BLOCK, HEADS, DH]))
                 nc.tensor.transpose(rden_ps[:, block], rden_rep[:].rearrange("n g d -> n (g d)"), identity[:])
+
+            for p in range(PIECES):
+                nodes = slice(p * NODES, (p + 1) * NODES)
+                in_block = slice((p % HALVES) * NODES, (p % HALVES + 1) * NODES)
+                score_ps = score_banks.tile([C, PIECE], F32, name="score_ps")
+                nc.tensor.matmul(
+                    score_ps[:], head_sb[:], prod[:, nodes, :].rearrange("c n t -> c (n t)"), start=True, stop=False
+                )
+                nc.tensor.matmul(
+                    score_ps[:],
+                    top_rep_of[p // HALVES][:].rearrange("n g d -> n (g d)"),
+                    minus_spread[:, in_block, :].rearrange("m n t -> m (n t)"),
+                    start=False, stop=True,
+                )
+                weight = weights.tile([C, NODES, K], F32, name="weight")
+                nc.scalar.activation(
+                    weight[:].rearrange("c n t -> c (n t)"), score_ps[:], ACT.Exp, scale=1.0 / math.sqrt(DH)
+                )
+                weight_of.append(weight)
 
             for first_piece, end_piece in ((0, PIECES - HALVES), (PIECES - HALVES, PIECES)):
                 columns = slice(first_piece * NODES, end_piece * NODES)

@@ -20,6 +20,7 @@ HEADS = C // DH
 BLOCK = 128
 BLOCKS = S // BLOCK
 HALVES = BLOCK // NODES
+PAIRS = BLOCKS // 2
 WARM_UP = 3
 
 FLOPS = 2 * C * (2 * C) * N + 2 * C * (2 * C) * S + 2 * C * C * N
@@ -30,6 +31,7 @@ def tile_attnno_kernel(tc, x, wkv, wqr, bqr, same_head, offs, out):
     with (
         tc.tile_pool(name="held", bufs=1) as held,
         tc.tile_pool(name="work", bufs=2) as work,
+        tc.tile_pool(name="weights", bufs=PIECES) as weights,
     ):
         offsets = held.tile([C, N // 16], U16, name="offsets")
         x_sb = held.tile([C, S], BF16, name="x_sb")
@@ -72,87 +74,68 @@ def tile_attnno_kernel(tc, x, wkv, wqr, bqr, same_head, offs, out):
         nc.scalar.activation(h[:], x_sb[:], ACT.Gelu)
 
         q = held.tile([C, S], F32, name="q")
-        res = held.tile([C, S], F32, name="res")
         prod = held.tile([C, S, K], BF16, name="prod")
         val = held.tile([C, S, K], F32, name="val")
-
-        with (
-            tc.psum_pool(name="plain_banks", bufs=1) as plain_banks,
-            tc.psum_pool(name="picked_banks", bufs=3) as picked_banks,
-        ):
-            q_ps = plain_banks.tile([C, S], F32, name="q_ps")
-            res_ps = plain_banks.tile([C, S], F32, name="res_ps")
-            nc.tensor.matmul(q_ps[:], wqr_sb[:, 0:C], h[:], start=True, stop=True)
-            nc.tensor.matmul(res_ps[:], wqr_sb[:, C : 2 * C], h[:], start=True, stop=True)
-            nc.scalar.activation(q[:], q_ps[:], ACT.Identity, bias=bias_q[:])
-            nc.scalar.activation(res[:], res_ps[:], ACT.Identity, bias=bias_res[:])
-
-            for p in range(PIECES):
-                nodes = slice(p * NODES, (p + 1) * NODES)
-                picked = h[:].indirect(offsets[:, p * (PIECE // 16) : (p + 1) * (PIECE // 16)])
-                key_ps = picked_banks.tile([C, PIECE], F32, name="key_ps")
-                val_ps = picked_banks.tile([C, PIECE], F32, name="val_ps")
-                nc.tensor.matmul(key_ps[:], wkv_sb[:, 0:C], picked, start=True, stop=True)
-                nc.tensor.matmul(val_ps[:], wkv_sb[:, C : 2 * C], picked, start=True, stop=True)
-                nc.vector.tensor_tensor(
-                    prod[:, nodes, :],
-                    key_ps[:].rearrange("c (n t) -> c n t", t=K),
-                    q[:, nodes].unsqueeze(2).to_broadcast([C, NODES, K]),
-                    ALU.mult,
-                )
-                nc.scalar.copy(val[:, nodes, :], val_ps[:].rearrange("c (n t) -> c n t", t=K))
-
         numer = held.tile([C, S], F32, name="numer")
         att = held.tile([C, S], F32, name="att")
         result = held.tile([C, S], F32, name="result")
 
         with (
-            tc.tile_pool(name="shifts", bufs=BLOCKS) as shifts,
-            tc.tile_pool(name="weights", bufs=PIECES) as weights,
+            tc.psum_pool(name="banks", bufs=4) as banks,
             tc.psum_pool(name="rden_bank", bufs=1) as rden_bank,
-            tc.psum_pool(name="by_node_banks", bufs=BLOCKS) as by_node_banks,
-            tc.psum_pool(name="score_banks", bufs=3) as score_banks,
+            tc.tile_pool(name="shifts", bufs=PAIRS) as shifts,
         ):
-            rden_ps = rden_bank.tile([C, S], F32, name="rden_ps")
-            top_rep_of = []
-            weight_of = []
+            def picked(p):
+                return h[:].indirect(offsets[:, p * (PIECE // 16) : (p + 1) * (PIECE // 16)])
 
-            for b in range(BLOCKS):
-                block = slice(b * BLOCK, (b + 1) * BLOCK)
+            def nodes_of(p):
+                return slice(p * NODES, (p + 1) * NODES)
 
-                by_node_ps = by_node_banks.tile([BLOCK, K, HEADS], F32, name="by_node_ps")
-                for t in range(K):
-                    nc.tensor.matmul(by_node_ps[:, t, :], prod[:, block, t], head_columns, start=True, stop=True)
-
-                top = work.tile([BLOCK, HEADS], F32, name="top")
-                nc.vector.tensor_reduce(top[:], by_node_ps[:].rearrange("n t g -> n g t"), X_AXIS, ALU.max)
-                top_rep = shifts.tile([BLOCK, HEADS, DH], BF16, name="top_rep")
-                nc.vector.tensor_copy(top_rep[:], top[:].unsqueeze(2).to_broadcast([BLOCK, HEADS, DH]))
-                top_rep_of.append(top_rep)
-
-                shifted = work.tile([BLOCK, K, HEADS], F32, name="shifted")
-                nc.vector.tensor_tensor(
-                    shifted[:], by_node_ps[:], top_rep[:, :, 0].unsqueeze(1).to_broadcast([BLOCK, K, HEADS]),
-                    ALU.subtract,
-                )
-                nc.scalar.activation(shifted[:], shifted[:], ACT.Exp, scale=1.0 / math.sqrt(DH))
-                rden_small = work.tile([BLOCK, HEADS], F32, name="rden_small")
-                nc.vector.tensor_reduce(rden_small[:], shifted[:].rearrange("n t g -> n g t"), X_AXIS, ALU.add)
-                nc.vector.reciprocal(rden_small[:], rden_small[:])
-                rden_rep = work.tile([BLOCK, HEADS, DH], F32, name="rden_rep")
-                nc.scalar.copy(rden_rep[:], rden_small[:].unsqueeze(2).to_broadcast([BLOCK, HEADS, DH]))
-                nc.tensor.transpose(rden_ps[:, block], rden_rep[:].rearrange("n g d -> n (g d)"), identity[:])
+            q_ps = banks.tile([C, S], F32, name="q_ps", tag="bank")
+            nc.tensor.matmul(q_ps[:], wqr_sb[:, 0:C], h[:], start=True, stop=True)
+            nc.scalar.activation(q[:], q_ps[:], ACT.Identity, bias=bias_q[:])
 
             for p in range(PIECES):
-                nodes = slice(p * NODES, (p + 1) * NODES)
+                key_ps = banks.tile([C, PIECE], F32, name="key_ps", tag="bank")
+                nc.tensor.matmul(key_ps[:], wkv_sb[:, 0:C], picked(p), start=True, stop=True)
+                nc.vector.tensor_tensor(
+                    prod[:, nodes_of(p), :],
+                    key_ps[:].rearrange("c (n t) -> c n t", t=K),
+                    q[:, nodes_of(p)].unsqueeze(2).to_broadcast([C, NODES, K]),
+                    ALU.mult,
+                )
+
+            by_node_of = []
+            top_rep_of = []
+            for a in range(PAIRS):
+                by_node_ps = banks.tile([BLOCK, 2, K, HEADS], F32, name="by_node_ps", tag="bank")
+                for i in range(2):
+                    b = 2 * a + i
+                    for t in range(K):
+                        nc.tensor.matmul(
+                            by_node_ps[:, i, t, :], prod[:, b * BLOCK : (b + 1) * BLOCK, t], head_columns,
+                            start=True, stop=True,
+                        )
+                top = work.tile([BLOCK, 2, HEADS], F32, name="top")
+                nc.vector.tensor_reduce(top[:], by_node_ps[:].rearrange("n i t g -> n i g t"), X_AXIS, ALU.max)
+                top_rep = shifts.tile([BLOCK, 2, HEADS, DH], BF16, name="top_rep")
+                nc.vector.tensor_copy(top_rep[:], top[:].unsqueeze(3).to_broadcast([BLOCK, 2, HEADS, DH]))
+                by_node_of.append(by_node_ps)
+                top_rep_of.append(top_rep)
+
+            weight_of = []
+
+            def weights_of_piece(p):
+                b = p // HALVES
                 in_block = slice((p % HALVES) * NODES, (p % HALVES + 1) * NODES)
-                score_ps = score_banks.tile([C, PIECE], F32, name="score_ps")
+                score_ps = banks.tile([C, PIECE], F32, name="score_ps", tag="bank")
                 nc.tensor.matmul(
-                    score_ps[:], head_sb[:], prod[:, nodes, :].rearrange("c n t -> c (n t)"), start=True, stop=False
+                    score_ps[:], head_sb[:], prod[:, nodes_of(p), :].rearrange("c n t -> c (n t)"),
+                    start=True, stop=False,
                 )
                 nc.tensor.matmul(
                     score_ps[:],
-                    top_rep_of[p // HALVES][:].rearrange("n g d -> n (g d)"),
+                    top_rep_of[b // 2][:, b % 2, :, :].rearrange("n g d -> n (g d)"),
                     minus_spread[:, in_block, :].rearrange("m n t -> m (n t)"),
                     start=False, stop=True,
                 )
@@ -162,14 +145,47 @@ def tile_attnno_kernel(tc, x, wkv, wqr, bqr, same_head, offs, out):
                 )
                 weight_of.append(weight)
 
+            for p in range(PIECES // 2):
+                weights_of_piece(p)
+
+            rden_ps = rden_bank.tile([C, S], F32, name="rden_ps")
+            for a in range(PAIRS):
+                shifted = work.tile([BLOCK, 2, K, HEADS], F32, name="shifted")
+                nc.vector.tensor_tensor(
+                    shifted[:], by_node_of[a][:],
+                    top_rep_of[a][:, :, :, 0].unsqueeze(2).to_broadcast([BLOCK, 2, K, HEADS]),
+                    ALU.subtract,
+                )
+                nc.scalar.activation(shifted[:], shifted[:], ACT.Exp, scale=1.0 / math.sqrt(DH))
+                rden_small = work.tile([BLOCK, 2, HEADS], F32, name="rden_small")
+                nc.vector.tensor_reduce(rden_small[:], shifted[:].rearrange("n i t g -> n i g t"), X_AXIS, ALU.add)
+                nc.vector.reciprocal(rden_small[:], rden_small[:])
+                rden_rep = work.tile([BLOCK, 2, HEADS, DH], F32, name="rden_rep")
+                nc.scalar.copy(rden_rep[:], rden_small[:].unsqueeze(3).to_broadcast([BLOCK, 2, HEADS, DH]))
+                for i in range(2):
+                    b = 2 * a + i
+                    nc.tensor.transpose(
+                        rden_ps[:, b * BLOCK : (b + 1) * BLOCK],
+                        rden_rep[:, i, :, :].rearrange("n g d -> n (g d)"), identity[:],
+                    )
+
+            for p in range(PIECES):
+                val_ps = banks.tile([C, PIECE], F32, name="val_ps", tag="bank")
+                nc.tensor.matmul(val_ps[:], wkv_sb[:, C : 2 * C], picked(p), start=True, stop=True)
+                nc.scalar.copy(val[:, nodes_of(p), :], val_ps[:].rearrange("c (n t) -> c n t", t=K))
+
+            for p in range(PIECES // 2, PIECES):
+                weights_of_piece(p)
+            res_ps = banks.tile([C, S], F32, name="res_ps", tag="bank")
+            nc.tensor.matmul(res_ps[:], wqr_sb[:, C : 2 * C], h[:], start=True, stop=True)
+
             for first_piece, end_piece in ((0, PIECES - HALVES), (PIECES - HALVES, PIECES)):
                 columns = slice(first_piece * NODES, end_piece * NODES)
                 for p in range(first_piece, end_piece):
-                    nodes = slice(p * NODES, (p + 1) * NODES)
                     weighted = work.tile([C, NODES, K], F32, name="weighted")
-                    nc.vector.tensor_tensor(weighted[:], weight_of[p][:], val[:, nodes, :], ALU.mult)
-                    nc.vector.tensor_reduce(numer[:, nodes], weighted[:], X_AXIS, ALU.add)
+                    nc.vector.tensor_tensor(weighted[:], weight_of[p][:], val[:, nodes_of(p), :], ALU.mult)
+                    nc.vector.tensor_reduce(numer[:, nodes_of(p)], weighted[:], X_AXIS, ALU.add)
                 nc.vector.tensor_tensor(att[:, columns], numer[:, columns], rden_ps[:, columns], ALU.mult)
-                nc.vector.tensor_tensor(att[:, columns], att[:, columns], res[:, columns], ALU.add)
-                nc.scalar.activation(result[:, columns], att[:, columns], ACT.Gelu)
+                nc.vector.tensor_tensor(att[:, columns], att[:, columns], res_ps[:, columns], ALU.add)
+                nc.scalar.activation(result[:, columns], att[:, columns], ACT.Gelu, bias=bias_res[:])
                 nc.sync.dma_start(out[:, columns], result[:, columns])

@@ -81,7 +81,7 @@ def tile_attnno_kernel(tc, x, wkv, wqr, bqr, same_head, offs, out):
         result = held.tile([C, S], F32, name="result")
 
         with (
-            tc.psum_pool(name="banks", bufs=4) as banks,
+            tc.psum_pool(name="banks", bufs=6) as banks,
             tc.psum_pool(name="rden_bank", bufs=1) as rden_bank,
             tc.tile_pool(name="shifts", bufs=PAIRS) as shifts,
         ):
@@ -148,17 +148,36 @@ def tile_attnno_kernel(tc, x, wkv, wqr, bqr, same_head, offs, out):
             for p in range(PIECES // 2):
                 weights_of_piece(p)
 
-            rden_ps = rden_bank.tile([C, S], F32, name="rden_ps")
+            small_exp_of = []
             for a in range(PAIRS):
-                shifted = work.tile([BLOCK, 2, K, HEADS], F32, name="shifted")
+                small_exp = shifts.tile([BLOCK, 2, K, HEADS], F32, name="small_exp")
                 nc.vector.tensor_tensor(
-                    shifted[:], by_node_of[a][:],
+                    small_exp[:], by_node_of[a][:],
                     top_rep_of[a][:, :, :, 0].unsqueeze(2).to_broadcast([BLOCK, 2, K, HEADS]),
                     ALU.subtract,
                 )
-                nc.scalar.activation(shifted[:], shifted[:], ACT.Exp, scale=1.0 / math.sqrt(DH))
+                nc.scalar.activation(small_exp[:], small_exp[:], ACT.Exp, scale=1.0 / math.sqrt(DH))
+                small_exp_of.append(small_exp)
+
+            def weighted_sum(p, values):
+                weighted = work.tile([C, NODES, K], F32, name="weighted")
+                nc.vector.tensor_tensor(weighted[:], weight_of[p][:], values, ALU.mult)
+                nc.vector.tensor_reduce(numer[:, nodes_of(p)], weighted[:], X_AXIS, ALU.add)
+
+            for p in range(PIECES):
+                val_ps = banks.tile([C, PIECE], F32, name="val_ps", tag="bank")
+                nc.tensor.matmul(val_ps[:], wkv_sb[:, C : 2 * C], picked(p), start=True, stop=True)
+                if p < PIECES // 2:
+                    weighted_sum(p, val_ps[:].rearrange("c (n t) -> c n t", t=K))
+                else:
+                    nc.scalar.copy(val[:, nodes_of(p), :], val_ps[:].rearrange("c (n t) -> c n t", t=K))
+
+            rden_ps = rden_bank.tile([C, S], F32, name="rden_ps")
+            for a in range(PAIRS):
                 rden_small = work.tile([BLOCK, 2, HEADS], F32, name="rden_small")
-                nc.vector.tensor_reduce(rden_small[:], shifted[:].rearrange("n i t g -> n i g t"), X_AXIS, ALU.add)
+                nc.vector.tensor_reduce(
+                    rden_small[:], small_exp_of[a][:].rearrange("n i t g -> n i g t"), X_AXIS, ALU.add
+                )
                 nc.vector.reciprocal(rden_small[:], rden_small[:])
                 rden_rep = work.tile([BLOCK, 2, HEADS, DH], F32, name="rden_rep")
                 nc.scalar.copy(rden_rep[:], rden_small[:].unsqueeze(3).to_broadcast([BLOCK, 2, HEADS, DH]))
@@ -169,11 +188,6 @@ def tile_attnno_kernel(tc, x, wkv, wqr, bqr, same_head, offs, out):
                         rden_rep[:, i, :, :].rearrange("n g d -> n (g d)"), identity[:],
                     )
 
-            for p in range(PIECES):
-                val_ps = banks.tile([C, PIECE], F32, name="val_ps", tag="bank")
-                nc.tensor.matmul(val_ps[:], wkv_sb[:, C : 2 * C], picked(p), start=True, stop=True)
-                nc.scalar.copy(val[:, nodes_of(p), :], val_ps[:].rearrange("c (n t) -> c n t", t=K))
-
             for p in range(PIECES // 2, PIECES):
                 weights_of_piece(p)
             res_ps = banks.tile([C, S], F32, name="res_ps", tag="bank")
@@ -181,10 +195,8 @@ def tile_attnno_kernel(tc, x, wkv, wqr, bqr, same_head, offs, out):
 
             for first_piece, end_piece in ((0, PIECES - HALVES), (PIECES - HALVES, PIECES)):
                 columns = slice(first_piece * NODES, end_piece * NODES)
-                for p in range(first_piece, end_piece):
-                    weighted = work.tile([C, NODES, K], F32, name="weighted")
-                    nc.vector.tensor_tensor(weighted[:], weight_of[p][:], val[:, nodes_of(p), :], ALU.mult)
-                    nc.vector.tensor_reduce(numer[:, nodes_of(p)], weighted[:], X_AXIS, ALU.add)
+                for p in range(max(first_piece, PIECES // 2), end_piece):
+                    weighted_sum(p, val[:, nodes_of(p), :])
                 nc.vector.tensor_tensor(att[:, columns], numer[:, columns], rden_ps[:, columns], ALU.mult)
                 nc.vector.tensor_tensor(att[:, columns], att[:, columns], res_ps[:, columns], ALU.add)
                 nc.scalar.activation(result[:, columns], att[:, columns], ACT.Gelu, bias=bias_res[:])

@@ -21,6 +21,8 @@ BLOCK = 128
 BLOCKS = S // BLOCK
 HALVES = BLOCK // NODES
 PAIRS = BLOCKS // 2
+EARLY = 5
+HELPED = (2, 3)
 WARM_UP = 3
 
 FLOPS = 2 * C * (2 * C) * N + 2 * C * (2 * C) * S + 2 * C * C * N
@@ -31,6 +33,7 @@ def tile_attnno_kernel(tc, x, wkv, wqr, bqr, same_head, offs, out):
     with (
         tc.tile_pool(name="held", bufs=1) as held,
         tc.tile_pool(name="work", bufs=2) as work,
+        tc.tile_pool(name="helpers", bufs=2) as helpers,
         tc.tile_pool(name="weights", bufs=PIECES) as weights,
     ):
         offsets = held.tile([C, N // 16], U16, name="offsets")
@@ -145,7 +148,7 @@ def tile_attnno_kernel(tc, x, wkv, wqr, bqr, same_head, offs, out):
                 )
                 weight_of.append(weight)
 
-            for p in range(PIECES // 2):
+            for p in range(EARLY):
                 weights_of_piece(p)
 
             small_exp_of = []
@@ -164,13 +167,25 @@ def tile_attnno_kernel(tc, x, wkv, wqr, bqr, same_head, offs, out):
                 nc.vector.tensor_tensor(weighted[:], weight_of[p][:], values, ALU.mult)
                 nc.vector.tensor_reduce(numer[:, nodes_of(p)], weighted[:], X_AXIS, ALU.add)
 
+            helped_of = {}
             for p in range(PIECES):
                 val_ps = banks.tile([C, PIECE], F32, name="val_ps", tag="bank")
                 nc.tensor.matmul(val_ps[:], wkv_sb[:, C : 2 * C], picked(p), start=True, stop=True)
-                if p < PIECES // 2:
+                if p < EARLY and p not in HELPED:
                     weighted_sum(p, val_ps[:].rearrange("c (n t) -> c n t", t=K))
                 else:
                     nc.scalar.copy(val[:, nodes_of(p), :], val_ps[:].rearrange("c (n t) -> c n t", t=K))
+                if p in HELPED:
+                    helped = helpers.tile([C, NODES, K], F32, name="helped")
+                    nc.gpsimd.tensor_tensor(helped[:], weight_of[p][:], val[:, nodes_of(p), :], ALU.mult)
+                    helped_of[p] = helped
+            for p in HELPED:
+                nc.vector.tensor_reduce(numer[:, nodes_of(p)], helped_of[p][:], X_AXIS, ALU.add)
+
+            for p in range(EARLY, PIECES):
+                weights_of_piece(p)
+            res_ps = banks.tile([C, S], F32, name="res_ps", tag="bank")
+            nc.tensor.matmul(res_ps[:], wqr_sb[:, C : 2 * C], h[:], start=True, stop=True)
 
             rden_ps = rden_bank.tile([C, S], F32, name="rden_ps")
             for a in range(PAIRS):
@@ -188,14 +203,9 @@ def tile_attnno_kernel(tc, x, wkv, wqr, bqr, same_head, offs, out):
                         rden_rep[:, i, :, :].rearrange("n g d -> n (g d)"), identity[:],
                     )
 
-            for p in range(PIECES // 2, PIECES):
-                weights_of_piece(p)
-            res_ps = banks.tile([C, S], F32, name="res_ps", tag="bank")
-            nc.tensor.matmul(res_ps[:], wqr_sb[:, C : 2 * C], h[:], start=True, stop=True)
-
             for first_piece, end_piece in ((0, PIECES - HALVES), (PIECES - HALVES, PIECES)):
                 columns = slice(first_piece * NODES, end_piece * NODES)
-                for p in range(max(first_piece, PIECES // 2), end_piece):
+                for p in range(max(first_piece, EARLY), end_piece):
                     weighted_sum(p, val[:, nodes_of(p), :])
                 nc.vector.tensor_tensor(att[:, columns], numer[:, columns], rden_ps[:, columns], ALU.mult)
                 nc.vector.tensor_tensor(att[:, columns], att[:, columns], res_ps[:, columns], ALU.add)

@@ -21,8 +21,8 @@ BLOCK = 128
 BLOCKS = S // BLOCK
 HALVES = BLOCK // NODES
 PAIRS = BLOCKS // 2
-EARLY = 5
-HELPED = (2, 3)
+EARLY = 4
+HELPED = (2, 3, 5)
 WARM_UP = 3
 
 FLOPS = 2 * C * (2 * C) * N + 2 * C * (2 * C) * S + 2 * C * C * N
@@ -33,7 +33,7 @@ def tile_attnno_kernel(tc, x, wkv, wqr, bqr, same_head, offs, out):
     with (
         tc.tile_pool(name="held", bufs=1) as held,
         tc.tile_pool(name="work", bufs=2) as work,
-        tc.tile_pool(name="helpers", bufs=2) as helpers,
+        tc.tile_pool(name="helpers", bufs=3) as helpers,
         tc.tile_pool(name="weights", bufs=PIECES) as weights,
     ):
         offsets = held.tile([C, N // 16], U16, name="offsets")
@@ -168,22 +168,35 @@ def tile_attnno_kernel(tc, x, wkv, wqr, bqr, same_head, offs, out):
                 nc.vector.tensor_reduce(numer[:, nodes_of(p)], weighted[:], X_AXIS, ALU.add)
 
             helped_of = {}
+            val_of = {}
+
+            def help_with(p):
+                helped = helpers.tile([C, NODES, K], F32, name="helped")
+                nc.gpsimd.tensor_tensor(helped[:], weight_of[p][:], val[:, nodes_of(p), :], ALU.mult)
+                helped_of[p] = helped
+
+            def sum_helped(p):
+                nc.vector.tensor_reduce(numer[:, nodes_of(p)], helped_of[p][:], X_AXIS, ALU.add)
+
             for p in range(PIECES):
                 val_ps = banks.tile([C, PIECE], F32, name="val_ps", tag="bank")
                 nc.tensor.matmul(val_ps[:], wkv_sb[:, C : 2 * C], picked(p), start=True, stop=True)
-                if p < EARLY and p not in HELPED:
-                    weighted_sum(p, val_ps[:].rearrange("c (n t) -> c n t", t=K))
-                else:
-                    nc.scalar.copy(val[:, nodes_of(p), :], val_ps[:].rearrange("c (n t) -> c n t", t=K))
+                val_of[p] = val_ps[:].rearrange("c (n t) -> c n t", t=K)
                 if p in HELPED:
-                    helped = helpers.tile([C, NODES, K], F32, name="helped")
-                    nc.gpsimd.tensor_tensor(helped[:], weight_of[p][:], val[:, nodes_of(p), :], ALU.mult)
-                    helped_of[p] = helped
+                    nc.scalar.copy(val[:, nodes_of(p), :], val_of[p])
+                if p < EARLY:
+                    if p in HELPED:
+                        help_with(p)
+                    else:
+                        weighted_sum(p, val_of[p])
             for p in HELPED:
-                nc.vector.tensor_reduce(numer[:, nodes_of(p)], helped_of[p][:], X_AXIS, ALU.add)
+                if p < EARLY:
+                    sum_helped(p)
 
             for p in range(EARLY, PIECES):
                 weights_of_piece(p)
+                if p in HELPED:
+                    help_with(p)
             res_ps = banks.tile([C, S], F32, name="res_ps", tag="bank")
             nc.tensor.matmul(res_ps[:], wqr_sb[:, C : 2 * C], h[:], start=True, stop=True)
 
@@ -203,10 +216,13 @@ def tile_attnno_kernel(tc, x, wkv, wqr, bqr, same_head, offs, out):
                         rden_rep[:, i, :, :].rearrange("n g d -> n (g d)"), identity[:],
                     )
 
+            weighted_sum(4, val_of[4])
+            weighted_sum(6, val_of[6])
+            sum_helped(5)
             for first_piece, end_piece in ((0, PIECES - HALVES), (PIECES - HALVES, PIECES)):
                 columns = slice(first_piece * NODES, end_piece * NODES)
-                for p in range(max(first_piece, EARLY), end_piece):
-                    weighted_sum(p, val[:, nodes_of(p), :])
+                if end_piece == PIECES:
+                    weighted_sum(7, val_of[7])
                 nc.vector.tensor_tensor(att[:, columns], numer[:, columns], rden_ps[:, columns], ALU.mult)
                 nc.vector.tensor_tensor(att[:, columns], att[:, columns], res_ps[:, columns], ALU.add)
                 nc.scalar.activation(result[:, columns], att[:, columns], ACT.Gelu, bias=bias_res[:])

@@ -21,8 +21,8 @@ BLOCK = 128
 BLOCKS = S // BLOCK
 HALVES = BLOCK // NODES
 PAIRS = BLOCKS // 2
-EARLY = 4
-HELPED = (2, 3, 5)
+EARLY = 5
+HELPED = (2, 3, 6)
 WARM_UP = 3
 
 FLOPS = 2 * C * (2 * C) * N + 2 * C * (2 * C) * S + 2 * C * C * N
@@ -216,13 +216,12 @@ def tile_attnno_kernel(tc, x, wkv, wqr, bqr, same_head, offs, out):
                         rden_rep[:, i, :, :].rearrange("n g d -> n (g d)"), identity[:],
                     )
 
-            weighted_sum(4, val_of[4])
-            weighted_sum(6, val_of[6])
-            sum_helped(5)
+            weighted_sum(5, val_of[5])
             for first_piece, end_piece in ((0, PIECES - HALVES), (PIECES - HALVES, PIECES)):
                 columns = slice(first_piece * NODES, end_piece * NODES)
                 if end_piece == PIECES:
                     weighted_sum(7, val_of[7])
+                    sum_helped(6)
                 nc.vector.tensor_tensor(att[:, columns], numer[:, columns], rden_ps[:, columns], ALU.mult)
                 nc.vector.tensor_tensor(att[:, columns], att[:, columns], res_ps[:, columns], ALU.add)
                 nc.scalar.activation(result[:, columns], att[:, columns], ACT.Gelu, bias=bias_res[:])

@@ -23,7 +23,6 @@ HALVES = BLOCK // NODES
 PAIRS = BLOCKS // 2
 EARLY = 5
 HELPED = (2, 3, 6)
-WARM_UP = 3
 
 FLOPS = 2 * C * (2 * C) * N + 2 * C * (2 * C) * S + 2 * C * C * N
 
@@ -50,13 +49,6 @@ def tile_attnno_kernel(tc, x, wkv, wqr, bqr, same_head, offs, out):
         nc.sync.dma_start(bias_q[:], bqr[0:C, :])
         nc.sync.dma_start(bias_res[:], bqr[C : 2 * C, :])
         nc.sync.dma_start(head_sb[:], same_head)
-
-        zeros = held.tile([C, S], BF16, name="zeros")
-        nc.gpsimd.memset(zeros[:], 0.0)
-        with tc.psum_pool(name="warm_bank", bufs=1) as warm_bank:
-            warm_ps = warm_bank.tile([C, S], F32, name="warm_ps")
-            for i in range(WARM_UP):
-                nc.tensor.matmul(warm_ps[:], zeros[:, 0:C], zeros[:], start=True, stop=True)
 
         identity = held.tile([BLOCK, BLOCK], F32, name="identity")
         make_identity(nc, identity[:])

@@ -69,7 +69,7 @@ def tile_attnno_kernel(tc, x, wkv, wqr, bqr, same_head, offs, out):
         nc.scalar.activation(h[:], x_sb[:], ACT.Gelu)
 
         q = held.tile([C, S], F32, name="q")
-        prod = held.tile([C, S, K], BF16, name="prod")
+        prod = held.tile([C, K, S], BF16, name="prod")
         val = held.tile([C, S, K], F32, name="val")
         numer = held.tile([C, S], F32, name="numer")
         att = held.tile([C, S], F32, name="att")
@@ -94,9 +94,9 @@ def tile_attnno_kernel(tc, x, wkv, wqr, bqr, same_head, offs, out):
                 key_ps = banks.tile([C, PIECE], F32, name="key_ps", tag="bank")
                 nc.tensor.matmul(key_ps[:], wkv_sb[:, 0:C], picked(p), start=True, stop=True)
                 nc.vector.tensor_tensor(
-                    prod[:, nodes_of(p), :],
-                    key_ps[:].rearrange("c (n t) -> c n t", t=K),
-                    q[:, nodes_of(p)].unsqueeze(2).to_broadcast([C, NODES, K]),
+                    prod[:, :, nodes_of(p)],
+                    key_ps[:].rearrange("c (n t) -> c t n", t=K),
+                    q[:, nodes_of(p)].unsqueeze(1).to_broadcast([C, K, NODES]),
                     ALU.mult,
                 )
 
@@ -108,7 +108,7 @@ def tile_attnno_kernel(tc, x, wkv, wqr, bqr, same_head, offs, out):
                     b = 2 * a + i
                     for t in range(K):
                         nc.tensor.matmul(
-                            by_node_ps[:, i, t, :], prod[:, b * BLOCK : (b + 1) * BLOCK, t], head_columns,
+                            by_node_ps[:, i, t, :], prod[:, t, b * BLOCK : (b + 1) * BLOCK], head_columns,
                             start=True, stop=True,
                         )
                 top = work.tile([BLOCK, 2, HEADS], F32, name="top")
@@ -125,7 +125,7 @@ def tile_attnno_kernel(tc, x, wkv, wqr, bqr, same_head, offs, out):
                 in_block = slice((p % HALVES) * NODES, (p % HALVES + 1) * NODES)
                 score_ps = banks.tile([C, PIECE], F32, name="score_ps", tag="bank")
                 nc.tensor.matmul(
-                    score_ps[:], head_sb[:], prod[:, nodes_of(p), :].rearrange("c n t -> c (n t)"),
+                    score_ps[:].rearrange("c (n t) -> c t n", t=K), head_sb[:], prod[:, :, nodes_of(p)],
                     start=True, stop=False,
                 )
                 nc.tensor.matmul(

@@ -40,14 +40,14 @@ def tile_attnno_kernel(tc, x, wkv, wqr, bqr, same_head, offs, out):
         wkv_sb = held.tile([C, 2 * C], BF16, name="wkv_sb")
         wqr_sb = held.tile([C, 2 * C], BF16, name="wqr_sb")
         head_sb = held.tile([C, C], BF16, name="head_sb")
-        bias_q = held.tile([C, 1], F32, name="bias_q")
-        bias_res = held.tile([C, 1], F32, name="bias_res")
+        biases = held.tile([C, 2], F32, name="biases")
+        bias_q = biases[:, 0:1]
+        bias_res = biases[:, 1:2]
         nc.scalar.dma_start(x_sb[:], x)
+        nc.sync.dma_start(biases[:], bqr.rearrange("(a p) o -> p (a o)", p=C))
         nc.sync.dma_start(wqr_sb[:], wqr)
         nc.sync.dma_start(offsets[:], offs)
         nc.sync.dma_start(wkv_sb[:], wkv)
-        nc.sync.dma_start(bias_q[:], bqr[0:C, :])
-        nc.sync.dma_start(bias_res[:], bqr[C : 2 * C, :])
         nc.sync.dma_start(head_sb[:], same_head)
 
         identity = held.tile([BLOCK, BLOCK], F32, name="identity")
@@ -88,7 +88,7 @@ def tile_attnno_kernel(tc, x, wkv, wqr, bqr, same_head, offs, out):
 
             q_ps = banks.tile([C, S], F32, name="q_ps", tag="bank")
             nc.tensor.matmul(q_ps[:], wqr_sb[:, 0:C], h[:], start=True, stop=True)
-            nc.scalar.activation(q[:], q_ps[:], ACT.Identity, bias=bias_q[:])
+            nc.scalar.activation(q[:], q_ps[:], ACT.Identity, bias=bias_q)
 
             for p in range(PIECES):
                 key_ps = banks.tile([C, PIECE], F32, name="key_ps", tag="bank")
@@ -216,5 +216,5 @@ def tile_attnno_kernel(tc, x, wkv, wqr, bqr, same_head, offs, out):
                     sum_helped(6)
                 nc.vector.tensor_tensor(att[:, columns], numer[:, columns], rden_ps[:, columns], ALU.mult)
                 nc.vector.tensor_tensor(att[:, columns], att[:, columns], res_ps[:, columns], ALU.add)
-                nc.scalar.activation(result[:, columns], att[:, columns], ACT.Gelu, bias=bias_res[:])
+                nc.scalar.activation(result[:, columns], att[:, columns], ACT.Gelu, bias=bias_res)
                 nc.sync.dma_start(out[:, columns], result[:, columns])

@@ -19,10 +19,10 @@ PIECES = N // PIECE
 HEADS = C // DH
 BLOCK = 128
 BLOCKS = S // BLOCK
-HALVES = BLOCK // NODES
-PAIRS = BLOCKS // 2
-EARLY = 5
-HELPED = (2, 3, 6)
+PAIR = 2
+PER_BLOCK = BLOCK // NODES
+PER_BANK = 4
+HELPED = (0, 1)
 
 FLOPS = 2 * C * (2 * C) * N + 2 * C * (2 * C) * S + 2 * C * C * N
 
@@ -32,8 +32,8 @@ def tile_attnno_kernel(tc, x, wkv, wqr, bqr, same_head, offs, out):
     with (
         tc.tile_pool(name="held", bufs=1) as held,
         tc.tile_pool(name="work", bufs=2) as work,
-        tc.tile_pool(name="helpers", bufs=3) as helpers,
-        tc.tile_pool(name="weights", bufs=PIECES) as weights,
+        tc.psum_pool(name="banks", bufs=3) as banks,
+        tc.psum_pool(name="turned_banks", bufs=5) as turned_banks,
     ):
         offsets = held.tile([C, N // 16], U16, name="offsets")
         x_sb = held.tile([C, S], BF16, name="x_sb")
@@ -52,17 +52,6 @@ def tile_attnno_kernel(tc, x, wkv, wqr, bqr, same_head, offs, out):
 
         identity = held.tile([BLOCK, BLOCK], F32, name="identity")
         make_identity(nc, identity[:])
-        minus_spread = held.tile([BLOCK, BLOCK, K], BF16, name="minus_spread")
-        nc.gpsimd.memset(minus_spread[:], 0.0)
-        nc.gpsimd.affine_select(
-            out=minus_spread[:].rearrange("m n t -> m (n t)"),
-            in_=minus_spread[:].rearrange("m n t -> m (n t)"),
-            pattern=[[-1, BLOCK], [0, K]],
-            compare_op=ALU.not_equal,
-            fill=-1.0,
-            base=0,
-            channel_multiplier=1,
-        )
         head_columns = head_sb[:].rearrange("e (g d) -> e g d", d=DH)[:, :, 0]
 
         h = held.tile([C, S], BF16, name="h")
@@ -70,151 +59,110 @@ def tile_attnno_kernel(tc, x, wkv, wqr, bqr, same_head, offs, out):
 
         q = held.tile([C, S], F32, name="q")
         prod = held.tile([C, K, S], BF16, name="prod")
-        val = held.tile([C, S, K], F32, name="val")
-        numer = held.tile([C, S], F32, name="numer")
-        att = held.tile([C, S], F32, name="att")
+        val = held.tile([C, BLOCKS, K, BLOCK], F32, name="val")
         result = held.tile([C, S], F32, name="result")
 
-        with (
-            tc.psum_pool(name="banks", bufs=6) as banks,
-            tc.psum_pool(name="rden_bank", bufs=1) as rden_bank,
-            tc.tile_pool(name="shifts", bufs=PAIRS) as shifts,
-        ):
-            def picked(p):
-                return h[:].indirect(offsets[:, p * (PIECE // 16) : (p + 1) * (PIECE // 16)])
+        def nodes_of(p):
+            return slice(p * NODES, (p + 1) * NODES)
 
-            def nodes_of(p):
-                return slice(p * NODES, (p + 1) * NODES)
+        def gathered(weight_columns, p, name):
+            bank = banks.tile([C, PIECE], F32, name=name, tag="bank")
+            picked = h[:].indirect(offsets[:, p * (PIECE // 16) : (p + 1) * (PIECE // 16)])
+            nc.tensor.matmul(bank[:], wkv_sb[:, weight_columns], picked, start=True, stop=True)
+            return bank[:].rearrange("c (n t) -> c t n", t=K)
 
-            q_ps = banks.tile([C, S], F32, name="q_ps", tag="bank")
-            nc.tensor.matmul(q_ps[:], wqr_sb[:, 0:C], h[:], start=True, stop=True)
-            nc.scalar.activation(q[:], q_ps[:], ACT.Identity, bias=bias_q)
+        q_ps = banks.tile([C, S], F32, name="q_ps", tag="bank")
+        nc.tensor.matmul(q_ps[:], wqr_sb[:, 0:C], h[:], start=True, stop=True)
+        nc.scalar.activation(q[:], q_ps[:], ACT.Identity, bias=bias_q)
+        exp_table = held.tile([C, 1], F32, name="exp_table")
+        nc.scalar.activation(exp_table[:], bias_q, ACT.Exp)
 
-            for p in range(PIECES):
-                key_ps = banks.tile([C, PIECE], F32, name="key_ps", tag="bank")
-                nc.tensor.matmul(key_ps[:], wkv_sb[:, 0:C], picked(p), start=True, stop=True)
+        def values_of_piece(p):
+            value = gathered(slice(C, 2 * C), p, "val_ps")
+            b, k = divmod(p, PER_BLOCK)
+            nc.scalar.copy(val[:, b, :, k * NODES : (k + 1) * NODES], value)
+
+        for p in range(PIECES):
+            key = gathered(slice(0, C), p, "key_ps")
+            nc.vector.tensor_tensor(
+                prod[:, :, nodes_of(p)], key, q[:, nodes_of(p)].unsqueeze(1).to_broadcast([C, K, NODES]), ALU.mult
+            )
+
+        score_of = []
+        for half in range(BLOCKS // PAIR):
+            score_ps = banks.tile([BLOCK, PAIR, K, HEADS], F32, name="score_ps", tag="bank")
+            for i in range(PAIR):
+                b = half * PAIR + i
+                for t in range(K):
+                    nc.tensor.matmul(
+                        score_ps[:, i, t, :], prod[:, t, b * BLOCK : (b + 1) * BLOCK], head_columns,
+                        start=True, stop=True,
+                    )
+            score_of.append(score_ps[:].rearrange("n i t g -> n i g t"))
+
+        share_of = []
+        for score in score_of:
+            top = work.tile([BLOCK, PAIR, HEADS], F32, name="top")
+            nc.vector.tensor_reduce(top[:], score, X_AXIS, ALU.max)
+            share = work.tile([BLOCK, PAIR, HEADS, K], F32, name="share")
+            nc.vector.tensor_tensor(
+                share[:], score, top[:].unsqueeze(3).to_broadcast([BLOCK, PAIR, HEADS, K]), ALU.subtract
+            )
+            nc.scalar.activation(share[:], share[:], ACT.Exp, scale=1.0 / math.sqrt(DH))
+            rden = work.tile([BLOCK, PAIR, HEADS], F32, name="rden")
+            nc.vector.tensor_reduce(rden[:], share[:], X_AXIS, ALU.add)
+            nc.vector.reciprocal(rden[:], rden[:])
+            nc.vector.tensor_tensor(
+                share[:], share[:], rden[:].unsqueeze(3).to_broadcast([BLOCK, PAIR, HEADS, K]), ALU.mult
+            )
+            share_of.append(share)
+
+        def weighted_values(b):
+            halves = []
+            for first in range(0, K, PER_BANK):
+                turned_ps = turned_banks.tile([BLOCK, PER_BANK, C], F32, name="turned_ps")
+                for t in range(PER_BANK):
+                    nc.tensor.transpose(turned_ps[:, t, :], val[:, b, first + t, :], identity[:])
+                weighted = work.tile([BLOCK, PER_BANK, C], F32, name="weighted", tag="weighted%d" % first)
                 nc.vector.tensor_tensor(
-                    prod[:, :, nodes_of(p)],
-                    key_ps[:].rearrange("c (n t) -> c t n", t=K),
-                    q[:, nodes_of(p)].unsqueeze(1).to_broadcast([C, K, NODES]),
+                    weighted[:].rearrange("n t (g d) -> n t g d", d=DH),
+                    turned_ps[:].rearrange("n t (g d) -> n t g d", d=DH),
+                    share_of[b // PAIR][:, b % PAIR, :, first : first + PER_BANK].rearrange("n g t -> n t g")
+                    .unsqueeze(3).to_broadcast([BLOCK, PER_BANK, HEADS, DH]),
                     ALU.mult,
                 )
+                halves.append(weighted)
+            return halves
 
-            by_node_of = []
-            top_rep_of = []
-            for a in range(PAIRS):
-                by_node_ps = banks.tile([BLOCK, 2, K, HEADS], F32, name="by_node_ps", tag="bank")
-                for i in range(2):
-                    b = 2 * a + i
-                    for t in range(K):
-                        nc.tensor.matmul(
-                            by_node_ps[:, i, t, :], prod[:, t, b * BLOCK : (b + 1) * BLOCK], head_columns,
-                            start=True, stop=True,
-                        )
-                top = work.tile([BLOCK, 2, HEADS], F32, name="top")
-                nc.vector.tensor_reduce(top[:], by_node_ps[:].rearrange("n i t g -> n i g t"), X_AXIS, ALU.max)
-                top_rep = shifts.tile([BLOCK, 2, HEADS, DH], BF16, name="top_rep")
-                nc.vector.tensor_copy(top_rep[:], top[:].unsqueeze(3).to_broadcast([BLOCK, 2, HEADS, DH]))
-                by_node_of.append(by_node_ps)
-                top_rep_of.append(top_rep)
+        def sum_to_two(b, halves):
+            four = work.tile([BLOCK, PER_BANK, C], F32, name="four")
+            engine = nc.gpsimd if b in HELPED else nc.vector
+            engine.tensor_tensor(four[:], halves[0][:], halves[1][:], ALU.add)
+            two = held.tile([BLOCK, 2, C], F32, name="two%d" % b)
+            engine.tensor_tensor(two[:], four[:, 0:2, :], four[:, 2:4, :], ALU.add)
+            return two
 
-            weight_of = []
+        def mean_of_block(b, two):
+            columns = slice(b * BLOCK, (b + 1) * BLOCK)
+            nc.tensor.matmul(out_ps[:, columns], two[:, 0, :], identity[:], start=True, stop=False)
+            nc.tensor.matmul(out_ps[:, columns], two[:, 1, :], identity[:], start=False, stop=False)
+            nc.tensor.matmul(out_ps[:, columns], wqr_sb[:, C : 2 * C], h[:, columns], start=False, stop=True)
 
-            def weights_of_piece(p):
-                b = p // HALVES
-                in_block = slice((p % HALVES) * NODES, (p % HALVES + 1) * NODES)
-                score_ps = banks.tile([C, PIECE], F32, name="score_ps", tag="bank")
-                nc.tensor.matmul(
-                    score_ps[:].rearrange("c (n t) -> c t n", t=K), head_sb[:], prod[:, :, nodes_of(p)],
-                    start=True, stop=False,
-                )
-                nc.tensor.matmul(
-                    score_ps[:],
-                    top_rep_of[b // 2][:, b % 2, :, :].rearrange("n g d -> n (g d)"),
-                    minus_spread[:, in_block, :].rearrange("m n t -> m (n t)"),
-                    start=False, stop=True,
-                )
-                weight = weights.tile([C, NODES, K], F32, name="weight")
-                nc.scalar.activation(
-                    weight[:].rearrange("c n t -> c (n t)"), score_ps[:], ACT.Exp, scale=1.0 / math.sqrt(DH)
-                )
-                weight_of.append(weight)
+        halves_of = []
+        two_of = []
+        for b in range(BLOCKS + 1):
+            if b < BLOCKS:
+                for p in range(b * PER_BLOCK, (b + 1) * PER_BLOCK):
+                    values_of_piece(p)
+            if b > 0:
+                halves_of.append(weighted_values(b - 1))
+            if b > 1:
+                two_of.append(sum_to_two(b - 2, halves_of[b - 2]))
+        two_of.append(sum_to_two(BLOCKS - 1, halves_of[BLOCKS - 1]))
+        out_ps = banks.tile([C, S], F32, name="out_ps", tag="bank")
+        for b in range(BLOCKS):
+            mean_of_block(b, two_of[b])
 
-            for p in range(EARLY):
-                weights_of_piece(p)
-
-            small_exp_of = []
-            for a in range(PAIRS):
-                small_exp = shifts.tile([BLOCK, 2, K, HEADS], F32, name="small_exp")
-                nc.vector.tensor_tensor(
-                    small_exp[:], by_node_of[a][:],
-                    top_rep_of[a][:, :, :, 0].unsqueeze(2).to_broadcast([BLOCK, 2, K, HEADS]),
-                    ALU.subtract,
-                )
-                nc.scalar.activation(small_exp[:], small_exp[:], ACT.Exp, scale=1.0 / math.sqrt(DH))
-                small_exp_of.append(small_exp)
-
-            def weighted_sum(p, values):
-                weighted = work.tile([C, NODES, K], F32, name="weighted")
-                nc.vector.tensor_tensor(weighted[:], weight_of[p][:], values, ALU.mult)
-                nc.vector.tensor_reduce(numer[:, nodes_of(p)], weighted[:], X_AXIS, ALU.add)
-
-            helped_of = {}
-            val_of = {}
-
-            def help_with(p):
-                helped = helpers.tile([C, NODES, K], F32, name="helped")
-                nc.gpsimd.tensor_tensor(helped[:], weight_of[p][:], val[:, nodes_of(p), :], ALU.mult)
-                helped_of[p] = helped
-
-            def sum_helped(p):
-                nc.vector.tensor_reduce(numer[:, nodes_of(p)], helped_of[p][:], X_AXIS, ALU.add)
-
-            for p in range(PIECES):
-                val_ps = banks.tile([C, PIECE], F32, name="val_ps", tag="bank")
-                nc.tensor.matmul(val_ps[:], wkv_sb[:, C : 2 * C], picked(p), start=True, stop=True)
-                val_of[p] = val_ps[:].rearrange("c (n t) -> c n t", t=K)
-                if p in HELPED:
-                    nc.scalar.copy(val[:, nodes_of(p), :], val_of[p])
-                if p < EARLY:
-                    if p in HELPED:
-                        help_with(p)
-                    else:
-                        weighted_sum(p, val_of[p])
-            for p in HELPED:
-                if p < EARLY:
-                    sum_helped(p)
-
-            for p in range(EARLY, PIECES):
-                weights_of_piece(p)
-                if p in HELPED:
-                    help_with(p)
-            res_ps = banks.tile([C, S], F32, name="res_ps", tag="bank")
-            nc.tensor.matmul(res_ps[:], wqr_sb[:, C : 2 * C], h[:], start=True, stop=True)
-
-            rden_ps = rden_bank.tile([C, S], F32, name="rden_ps")
-            for a in range(PAIRS):
-                rden_small = work.tile([BLOCK, 2, HEADS], F32, name="rden_small")
-                nc.vector.tensor_reduce(
-                    rden_small[:], small_exp_of[a][:].rearrange("n i t g -> n i g t"), X_AXIS, ALU.add
-                )
-                nc.vector.reciprocal(rden_small[:], rden_small[:])
-                rden_rep = work.tile([BLOCK, 2, HEADS, DH], F32, name="rden_rep")
-                nc.scalar.copy(rden_rep[:], rden_small[:].unsqueeze(3).to_broadcast([BLOCK, 2, HEADS, DH]))
-                for i in range(2):
-                    b = 2 * a + i
-                    nc.tensor.transpose(
-                        rden_ps[:, b * BLOCK : (b + 1) * BLOCK],
-                        rden_rep[:, i, :, :].rearrange("n g d -> n (g d)"), identity[:],
-                    )
-
-            weighted_sum(5, val_of[5])
-            for first_piece, end_piece in ((0, PIECES - HALVES), (PIECES - HALVES, PIECES)):
-                columns = slice(first_piece * NODES, end_piece * NODES)
-                if end_piece == PIECES:
-                    weighted_sum(7, val_of[7])
-                    sum_helped(6)
-                nc.vector.tensor_tensor(att[:, columns], numer[:, columns], rden_ps[:, columns], ALU.mult)
-                nc.vector.tensor_tensor(att[:, columns], att[:, columns], res_ps[:, columns], ALU.add)
-                nc.scalar.activation(result[:, columns], att[:, columns], ACT.Gelu, bias=bias_res)
-                nc.sync.dma_start(out[:, columns], result[:, columns])
+        for columns in (slice(0, S - BLOCK), slice(S - BLOCK, S)):
+            nc.scalar.activation(result[:, columns], out_ps[:, columns], ACT.Gelu, bias=bias_res)
+            nc.sync.dma_start(out[:, columns], result[:, columns])

@@ -22,6 +22,7 @@ BLOCKS = S // BLOCK
 PAIR = 2
 PER_BLOCK = BLOCK // NODES
 PER_BANK = 4
+EARLY = 1
 HELPED = (0, 1)
 
 FLOPS = 2 * C * (2 * C) * N + 2 * C * (2 * C) * S + 2 * C * C * N
@@ -32,6 +33,7 @@ def tile_attnno_kernel(tc, x, wkv, wqr, bqr, same_head, offs, out):
     with (
         tc.tile_pool(name="held", bufs=1) as held,
         tc.tile_pool(name="work", bufs=2) as work,
+        tc.tile_pool(name="terms", bufs=BLOCKS) as terms,
         tc.psum_pool(name="banks", bufs=3) as banks,
         tc.psum_pool(name="turned_banks", bufs=5) as turned_banks,
     ):
@@ -87,6 +89,8 @@ def tile_attnno_kernel(tc, x, wkv, wqr, bqr, same_head, offs, out):
             nc.vector.tensor_tensor(
                 prod[:, :, nodes_of(p)], key, q[:, nodes_of(p)].unsqueeze(1).to_broadcast([C, K, NODES]), ALU.mult
             )
+        for p in range(EARLY):
+            values_of_piece(p)
 
         score_of = []
         for half in range(BLOCKS // PAIR):
@@ -123,7 +127,7 @@ def tile_attnno_kernel(tc, x, wkv, wqr, bqr, same_head, offs, out):
                 turned_ps = turned_banks.tile([BLOCK, PER_BANK, C], F32, name="turned_ps")
                 for t in range(PER_BANK):
                     nc.tensor.transpose(turned_ps[:, t, :], val[:, b, first + t, :], identity[:])
-                weighted = work.tile([BLOCK, PER_BANK, C], F32, name="weighted", tag="weighted%d" % first)
+                weighted = terms.tile([BLOCK, PER_BANK, C], F32, name="weighted", tag="weighted%d" % first)
                 nc.vector.tensor_tensor(
                     weighted[:].rearrange("n t (g d) -> n t g d", d=DH),
                     turned_ps[:].rearrange("n t (g d) -> n t g d", d=DH),
@@ -135,10 +139,10 @@ def tile_attnno_kernel(tc, x, wkv, wqr, bqr, same_head, offs, out):
             return halves
 
         def sum_to_two(b, halves):
-            four = work.tile([BLOCK, PER_BANK, C], F32, name="four")
+            four = terms.tile([BLOCK, PER_BANK, C], F32, name="four")
             engine = nc.gpsimd if b in HELPED else nc.vector
             engine.tensor_tensor(four[:], halves[0][:], halves[1][:], ALU.add)
-            two = held.tile([BLOCK, 2, C], F32, name="two%d" % b)
+            two = terms.tile([BLOCK, 2, C], F32, name="two")
             engine.tensor_tensor(two[:], four[:, 0:2, :], four[:, 2:4, :], ALU.add)
             return two
 
@@ -152,7 +156,7 @@ def tile_attnno_kernel(tc, x, wkv, wqr, bqr, same_head, offs, out):
         two_of = []
         for b in range(BLOCKS + 1):
             if b < BLOCKS:
-                for p in range(b * PER_BLOCK, (b + 1) * PER_BLOCK):
+                for p in range(max(EARLY, b * PER_BLOCK), (b + 1) * PER_BLOCK):
                     values_of_piece(p)
             if b > 0:
                 halves_of.append(weighted_values(b - 1))

@@ -46,10 +46,10 @@ def tile_attnno_kernel(tc, x, wkv, wqr, bqr, same_head, offs, out):
         bias_q = biases[:, 0:1]
         bias_res = biases[:, 1:2]
         nc.scalar.dma_start(x_sb[:], x)
-        nc.sync.dma_start(biases[:], bqr.rearrange("(a p) o -> p (a o)", p=C))
         nc.sync.dma_start(wqr_sb[:], wqr)
         nc.sync.dma_start(offsets[:], offs)
         nc.sync.dma_start(wkv_sb[:], wkv)
+        nc.sync.dma_start(biases[:], bqr.rearrange("(a p) o -> p (a o)", p=C))
         nc.sync.dma_start(head_sb[:], same_head)
 
         identity = held.tile([BLOCK, BLOCK], F32, name="identity")
@@ -77,7 +77,7 @@ def tile_attnno_kernel(tc, x, wkv, wqr, bqr, same_head, offs, out):
         nc.tensor.matmul(q_ps[:], wqr_sb[:, 0:C], h[:], start=True, stop=True)
         nc.scalar.activation(q[:], q_ps[:], ACT.Identity, bias=bias_q)
         exp_table = held.tile([C, 1], F32, name="exp_table")
-        nc.scalar.activation(exp_table[:], bias_q, ACT.Exp)
+        nc.scalar.activation(exp_table[:], q[:, 0:1], ACT.Exp, scale=0.0)
 
         def values_of_piece(p):
             value = gathered(slice(C, 2 * C), p, "val_ps")

@@ -121,51 +121,66 @@ def tile_attnno_kernel(tc, x, wkv, wqr, bqr, same_head, offs, out):
             )
             share_of.append(share)
 
-        def weighted_values(b):
-            halves = []
+        def turned_values(b, first, order):
+            turned_ps = turned_banks.tile([BLOCK, PER_BANK * C], F32, name="turned_ps")
+            for t in range(PER_BANK):
+                nc.tensor.transpose(
+                    turned_ps[:].rearrange(order, t=PER_BANK)[:, t, :], val[:, b, first + t, :], identity[:]
+                )
+            return turned_ps
+
+        def terms_by_gpsimd(b):
+            products = []
             for first in range(0, K, PER_BANK):
-                turned_ps = turned_banks.tile([BLOCK, PER_BANK, C], F32, name="turned_ps")
-                for t in range(PER_BANK):
-                    nc.tensor.transpose(turned_ps[:, t, :], val[:, b, first + t, :], identity[:])
+                turned_ps = turned_values(b, first, "n (t c) -> n t c")
                 weighted = terms.tile([BLOCK, PER_BANK, C], F32, name="weighted", tag="weighted%d" % first)
                 nc.vector.tensor_tensor(
                     weighted[:].rearrange("n t (g d) -> n t g d", d=DH),
-                    turned_ps[:].rearrange("n t (g d) -> n t g d", d=DH),
+                    turned_ps[:].rearrange("n (t g d) -> n t g d", t=PER_BANK, d=DH),
                     share_of[b // PAIR][:, b % PAIR, :, first : first + PER_BANK].rearrange("n g t -> n t g")
                     .unsqueeze(3).to_broadcast([BLOCK, PER_BANK, HEADS, DH]),
                     ALU.mult,
                 )
-                halves.append(weighted)
-            return halves
-
-        def sum_to_two(b, halves):
+                products.append(weighted)
             four = terms.tile([BLOCK, PER_BANK, C], F32, name="four")
-            engine = nc.gpsimd if b in HELPED else nc.vector
-            engine.tensor_tensor(four[:], halves[0][:], halves[1][:], ALU.add)
+            nc.gpsimd.tensor_tensor(four[:], products[0][:], products[1][:], ALU.add)
             two = terms.tile([BLOCK, 2, C], F32, name="two")
-            engine.tensor_tensor(two[:], four[:, 0:2, :], four[:, 2:4, :], ALU.add)
-            return two
+            nc.gpsimd.tensor_tensor(two[:], four[:, 0:2, :], four[:, 2:4, :], ALU.add)
+            return [two[:, 0, :], two[:, 1, :]]
 
-        def mean_of_block(b, two):
+        def terms_by_vector(b):
+            sums = []
+            for first in range(0, K, PER_BANK):
+                turned_ps = turned_values(b, first, "n (c t) -> n t c")
+                weighted = work.tile([BLOCK, C, PER_BANK], F32, name="weighted")
+                nc.vector.tensor_tensor(
+                    weighted[:].rearrange("n (g d) t -> n g d t", d=DH),
+                    turned_ps[:].rearrange("n (g d t) -> n g d t", d=DH, t=PER_BANK),
+                    share_of[b // PAIR][:, b % PAIR, :, first : first + PER_BANK]
+                    .unsqueeze(2).to_broadcast([BLOCK, HEADS, DH, PER_BANK]),
+                    ALU.mult,
+                )
+                part = terms.tile([BLOCK, C], F32, name="part", tag="part%d" % first)
+                nc.vector.tensor_reduce(part[:], weighted[:], X_AXIS, ALU.add)
+                sums.append(part[:])
+            return sums
+
+        def mean_of_block(b, last_terms):
             columns = slice(b * BLOCK, (b + 1) * BLOCK)
-            nc.tensor.matmul(out_ps[:, columns], two[:, 0, :], identity[:], start=True, stop=False)
-            nc.tensor.matmul(out_ps[:, columns], two[:, 1, :], identity[:], start=False, stop=False)
+            for i, term in enumerate(last_terms):
+                nc.tensor.matmul(out_ps[:, columns], term, identity[:], start=(i == 0), stop=False)
             nc.tensor.matmul(out_ps[:, columns], wqr_sb[:, C : 2 * C], h[:, columns], start=False, stop=True)
 
-        halves_of = []
-        two_of = []
+        terms_of = []
         for b in range(BLOCKS + 1):
             if b < BLOCKS:
                 for p in range(max(EARLY, b * PER_BLOCK), (b + 1) * PER_BLOCK):
                     values_of_piece(p)
             if b > 0:
-                halves_of.append(weighted_values(b - 1))
-            if b > 1:
-                two_of.append(sum_to_two(b - 2, halves_of[b - 2]))
-        two_of.append(sum_to_two(BLOCKS - 1, halves_of[BLOCKS - 1]))
+                terms_of.append(terms_by_gpsimd(b - 1) if b - 1 in HELPED else terms_by_vector(b - 1))
         out_ps = banks.tile([C, S], F32, name="out_ps", tag="bank")
-        for b in range(BLOCKS):
-            mean_of_block(b, two_of[b])
+        for b in (0, 2, 1, 3):
+            mean_of_block(b, terms_of[b])
 
         for columns in (slice(0, S - BLOCK), slice(S - BLOCK, S)):
             nc.scalar.activation(result[:, columns], out_ps[:, columns], ACT.Gelu, bias=bias_res)

@@ -121,22 +121,20 @@ def tile_attnno_kernel(tc, x, wkv, wqr, bqr, same_head, offs, out):
             )
             share_of.append(share)
 
-        def turned_values(b, first, order):
-            turned_ps = turned_banks.tile([BLOCK, PER_BANK * C], F32, name="turned_ps")
+        def turned_values(b, first):
+            turned_ps = turned_banks.tile([BLOCK, PER_BANK, C], F32, name="turned_ps")
             for t in range(PER_BANK):
-                nc.tensor.transpose(
-                    turned_ps[:].rearrange(order, t=PER_BANK)[:, t, :], val[:, b, first + t, :], identity[:]
-                )
-            return turned_ps
+                nc.tensor.transpose(turned_ps[:, t, :], val[:, b, first + t, :], identity[:])
+            return turned_ps[:].rearrange("n t (g d) -> n t g d", d=DH)
 
         def terms_by_gpsimd(b):
             products = []
             for first in range(0, K, PER_BANK):
-                turned_ps = turned_values(b, first, "n (t c) -> n t c")
+                turned = turned_values(b, first)
                 weighted = terms.tile([BLOCK, PER_BANK, C], F32, name="weighted", tag="weighted%d" % first)
                 nc.vector.tensor_tensor(
                     weighted[:].rearrange("n t (g d) -> n t g d", d=DH),
-                    turned_ps[:].rearrange("n (t g d) -> n t g d", t=PER_BANK, d=DH),
+                    turned,
                     share_of[b // PAIR][:, b % PAIR, :, first : first + PER_BANK].rearrange("n g t -> n t g")
                     .unsqueeze(3).to_broadcast([BLOCK, PER_BANK, HEADS, DH]),
                     ALU.mult,
@@ -151,11 +149,11 @@ def tile_attnno_kernel(tc, x, wkv, wqr, bqr, same_head, offs, out):
         def terms_by_vector(b):
             sums = []
             for first in range(0, K, PER_BANK):
-                turned_ps = turned_values(b, first, "n (c t) -> n t c")
+                turned = turned_values(b, first)
                 weighted = work.tile([BLOCK, C, PER_BANK], F32, name="weighted")
                 nc.vector.tensor_tensor(
                     weighted[:].rearrange("n (g d) t -> n g d t", d=DH),
-                    turned_ps[:].rearrange("n (g d t) -> n g d t", d=DH, t=PER_BANK),
+                    turned.rearrange("n t g d -> n g d t"),
                     share_of[b // PAIR][:, b % PAIR, :, first : first + PER_BANK]
                     .unsqueeze(2).to_broadcast([BLOCK, HEADS, DH, PER_BANK]),
                     ALU.mult,

@@ -45,7 +45,7 @@ def tile_attnno_kernel(tc, x, wkv, wqr, bqr, same_head, offs, out):
         biases = held.tile([C, 2], F32, name="biases")
         bias_q = biases[:, 0:1]
         bias_res = biases[:, 1:2]
-        nc.scalar.dma_start(x_sb[:], x)
+        nc.sync.dma_start(x_sb[:], x)
         nc.sync.dma_start(wqr_sb[:], wqr)
         nc.sync.dma_start(offsets[:], offs)
         nc.sync.dma_start(wkv_sb[:], wkv)

@@ -24,6 +24,7 @@ PER_BLOCK = BLOCK // NODES
 PER_BANK = 4
 EARLY = 1
 HELPED = (0, 1)
+UNSUMMED = (2, PER_BANK)
 
 FLOPS = 2 * C * (2 * C) * N + 2 * C * (2 * C) * S + 2 * C * C * N
 
@@ -82,7 +83,10 @@ def tile_attnno_kernel(tc, x, wkv, wqr, bqr, same_head, offs, out):
         def values_of_piece(p):
             value = gathered(slice(C, 2 * C), p, "val_ps")
             b, k = divmod(p, PER_BLOCK)
-            nc.scalar.copy(val[:, b, :, k * NODES : (k + 1) * NODES], value)
+            step = PER_BANK if p == PIECES - 1 else K
+            for first in range(0, K, step):
+                part = slice(first, first + step)
+                nc.scalar.copy(val[:, b, part, k * NODES : (k + 1) * NODES], value[:, part, :])
 
         for p in range(PIECES):
             key = gathered(slice(0, C), p, "key_ps")
@@ -121,47 +125,49 @@ def tile_attnno_kernel(tc, x, wkv, wqr, bqr, same_head, offs, out):
             )
             share_of.append(share)
 
-        def turned_values(b, first):
+        def weighted_values(b, first, t_inside):
             turned_ps = turned_banks.tile([BLOCK, PER_BANK, C], F32, name="turned_ps")
             for t in range(PER_BANK):
                 nc.tensor.transpose(turned_ps[:, t, :], val[:, b, first + t, :], identity[:])
-            return turned_ps[:].rearrange("n t (g d) -> n t g d", d=DH)
-
-        def terms_by_gpsimd(b):
-            products = []
-            for first in range(0, K, PER_BANK):
-                turned = turned_values(b, first)
+            turned = turned_ps[:].rearrange("n t (g d) -> n t g d", d=DH)
+            share = share_of[b // PAIR][:, b % PAIR, :, first : first + PER_BANK]
+            if t_inside:
+                weighted = terms.tile([BLOCK, C, PER_BANK], F32, name="weighted", tag="weighted%d" % first)
+                nc.vector.tensor_tensor(
+                    weighted[:].rearrange("n (g d) t -> n g d t", d=DH),
+                    turned.rearrange("n t g d -> n g d t"),
+                    share.unsqueeze(2).to_broadcast([BLOCK, HEADS, DH, PER_BANK]),
+                    ALU.mult,
+                )
+            else:
                 weighted = terms.tile([BLOCK, PER_BANK, C], F32, name="weighted", tag="weighted%d" % first)
                 nc.vector.tensor_tensor(
                     weighted[:].rearrange("n t (g d) -> n t g d", d=DH),
                     turned,
-                    share_of[b // PAIR][:, b % PAIR, :, first : first + PER_BANK].rearrange("n g t -> n t g")
-                    .unsqueeze(3).to_broadcast([BLOCK, PER_BANK, HEADS, DH]),
+                    share.rearrange("n g t -> n t g").unsqueeze(3).to_broadcast([BLOCK, PER_BANK, HEADS, DH]),
                     ALU.mult,
                 )
-                products.append(weighted)
-            four = terms.tile([BLOCK, PER_BANK, C], F32, name="four")
-            nc.gpsimd.tensor_tensor(four[:], products[0][:], products[1][:], ALU.add)
-            two = terms.tile([BLOCK, 2, C], F32, name="two")
-            nc.gpsimd.tensor_tensor(two[:], four[:, 0:2, :], four[:, 2:4, :], ALU.add)
-            return [two[:, 0, :], two[:, 1, :]]
+            return weighted
 
-        def terms_by_vector(b):
-            sums = []
+        def terms_of_block(b):
+            if b in HELPED:
+                products = [weighted_values(b, first, False) for first in range(0, K, PER_BANK)]
+                four = terms.tile([BLOCK, PER_BANK, C], F32, name="four")
+                nc.gpsimd.tensor_tensor(four[:], products[0][:], products[1][:], ALU.add)
+                two = terms.tile([BLOCK, 2, C], F32, name="two")
+                nc.gpsimd.tensor_tensor(two[:], four[:, 0:2, :], four[:, 2:4, :], ALU.add)
+                return [two[:, 0, :], two[:, 1, :]]
+            left = []
             for first in range(0, K, PER_BANK):
-                turned = turned_values(b, first)
-                weighted = work.tile([BLOCK, C, PER_BANK], F32, name="weighted")
-                nc.vector.tensor_tensor(
-                    weighted[:].rearrange("n (g d) t -> n g d t", d=DH),
-                    turned.rearrange("n t g d -> n g d t"),
-                    share_of[b // PAIR][:, b % PAIR, :, first : first + PER_BANK]
-                    .unsqueeze(2).to_broadcast([BLOCK, HEADS, DH, PER_BANK]),
-                    ALU.mult,
-                )
-                part = terms.tile([BLOCK, C], F32, name="part", tag="part%d" % first)
-                nc.vector.tensor_reduce(part[:], weighted[:], X_AXIS, ALU.add)
-                sums.append(part[:])
-            return sums
+                if (b, first) == UNSUMMED:
+                    weighted = weighted_values(b, first, False)
+                    left += [weighted[:, t, :] for t in range(PER_BANK)]
+                else:
+                    weighted = weighted_values(b, first, True)
+                    part = terms.tile([BLOCK, C], F32, name="part", tag="part%d" % first)
+                    nc.vector.tensor_reduce(part[:], weighted[:], X_AXIS, ALU.add)
+                    left.append(part[:])
+            return left
 
         def mean_of_block(b, last_terms):
             columns = slice(b * BLOCK, (b + 1) * BLOCK)
@@ -175,7 +181,7 @@ def tile_attnno_kernel(tc, x, wkv, wqr, bqr, same_head, offs, out):
                 for p in range(max(EARLY, b * PER_BLOCK), (b + 1) * PER_BLOCK):
                     values_of_piece(p)
             if b > 0:
-                terms_of.append(terms_by_gpsimd(b - 1) if b - 1 in HELPED else terms_by_vector(b - 1))
+                terms_of.append(terms_of_block(b - 1))
         out_ps = banks.tile([C, S], F32, name="out_ps", tag="bank")
         for b in (0, 2, 1, 3):
             mean_of_block(b, terms_of[b])

@@ -76,7 +76,8 @@ def tile_attnno_kernel(tc, x, wkv, wqr, bqr, same_head, offs, out):
 
         q_ps = banks.tile([C, S], F32, name="q_ps", tag="bank")
         nc.tensor.matmul(q_ps[:], wqr_sb[:, 0:C], h[:], start=True, stop=True)
-        nc.scalar.activation(q[:], q_ps[:], ACT.Identity, bias=bias_q)
+        for half in (slice(0, S // 2), slice(S // 2, S)):
+            nc.scalar.activation(q[:, half], q_ps[:, half], ACT.Identity, bias=bias_q)
         exp_table = held.tile([C, 1], F32, name="exp_table")
         nc.scalar.activation(exp_table[:], q[:, 0:1], ACT.Exp, scale=0.0)
 

import math

import concourse.mybir as mybir
from concourse.masks import make_identity

BF16, F32, U16 = mybir.dt.bfloat16, mybir.dt.float32, mybir.dt.uint16
ALU = mybir.AluOpType
ACT = mybir.ActivationFunctionType
X_AXIS = mybir.AxisListType.X

C = 128
S = 512
K = 8
DH = 16
N = S * K
PIECE = 512
NODES = PIECE // K
PIECES = N // PIECE
HEADS = C // DH
BLOCK = 128
BLOCKS = S // BLOCK
PAIR = 2
PER_BLOCK = BLOCK // NODES
PER_BANK = 4
EARLY = 1
HELPED = (0, 1)
UNSUMMED = (2, PER_BANK)

FLOPS = 2 * C * (2 * C) * N + 2 * C * (2 * C) * S + 2 * C * C * N


def tile_attnno_kernel(tc, x, wkv, wqr, bqr, same_head, offs, out):
    nc = tc.nc
    with (
        tc.tile_pool(name="held", bufs=1) as held,
        tc.tile_pool(name="work", bufs=2) as work,
        tc.tile_pool(name="terms", bufs=BLOCKS) as terms,
        tc.psum_pool(name="banks", bufs=3) as banks,
        tc.psum_pool(name="turned_banks", bufs=5) as turned_banks,
    ):
        offsets = held.tile([C, N // 16], U16, name="offsets")
        x_sb = held.tile([C, S], BF16, name="x_sb")
        wkv_sb = held.tile([C, 2 * C], BF16, name="wkv_sb")
        wqr_sb = held.tile([C, 2 * C], BF16, name="wqr_sb")
        head_sb = held.tile([C, C], BF16, name="head_sb")
        biases = held.tile([C, 2], F32, name="biases")
        bias_q = biases[:, 0:1]
        bias_res = biases[:, 1:2]
        nc.sync.dma_start(x_sb[:], x)
        nc.sync.dma_start(wqr_sb[:], wqr)
        nc.sync.dma_start(offsets[:], offs)
        nc.sync.dma_start(wkv_sb[:], wkv)
        nc.sync.dma_start(biases[:], bqr.rearrange("(a p) o -> p (a o)", p=C))
        nc.sync.dma_start(head_sb[:], same_head)

        identity = held.tile([BLOCK, BLOCK], F32, name="identity")
        make_identity(nc, identity[:])
        head_columns = head_sb[:].rearrange("e (g d) -> e g d", d=DH)[:, :, 0]

        h = held.tile([C, S], BF16, name="h")
        nc.scalar.activation(h[:], x_sb[:], ACT.Gelu)

        q = held.tile([C, S], F32, name="q")
        prod = held.tile([C, K, S], BF16, name="prod")
        val = held.tile([C, BLOCKS, K, BLOCK], F32, name="val")
        result = held.tile([C, S], F32, name="result")

        def nodes_of(p):
            return slice(p * NODES, (p + 1) * NODES)

        def gathered(weight_columns, p, name):
            bank = banks.tile([C, PIECE], F32, name=name, tag="bank")
            picked = h[:].indirect(offsets[:, p * (PIECE // 16) : (p + 1) * (PIECE // 16)])
            nc.tensor.matmul(bank[:], wkv_sb[:, weight_columns], picked, start=True, stop=True)
            return bank[:].rearrange("c (n t) -> c t n", t=K)

        q_ps = banks.tile([C, S], F32, name="q_ps", tag="bank")
        nc.tensor.matmul(q_ps[:], wqr_sb[:, 0:C], h[:], start=True, stop=True)
        for half in (slice(0, S // 2), slice(S // 2, S)):
            nc.scalar.activation(q[:, half], q_ps[:, half], ACT.Identity, bias=bias_q)
        exp_table = held.tile([C, 1], F32, name="exp_table")
        nc.scalar.activation(exp_table[:], q[:, 0:1], ACT.Exp, scale=0.0)

        def values_of_piece(p):
            value = gathered(slice(C, 2 * C), p, "val_ps")
            b, k = divmod(p, PER_BLOCK)
            step = PER_BANK if p == PIECES - 1 else K
            for first in range(0, K, step):
                part = slice(first, first + step)
                nc.scalar.copy(val[:, b, part, k * NODES : (k + 1) * NODES], value[:, part, :])

        for p in range(PIECES):
            key = gathered(slice(0, C), p, "key_ps")
            nc.vector.tensor_tensor(
                prod[:, :, nodes_of(p)], key, q[:, nodes_of(p)].unsqueeze(1).to_broadcast([C, K, NODES]), ALU.mult
            )
        for p in range(EARLY):
            values_of_piece(p)

        score_of = []
        for half in range(BLOCKS // PAIR):
            score_ps = banks.tile([BLOCK, PAIR, K, HEADS], F32, name="score_ps", tag="bank")
            for i in range(PAIR):
                b = half * PAIR + i
                for t in range(K):
                    nc.tensor.matmul(
                        score_ps[:, i, t, :], prod[:, t, b * BLOCK : (b + 1) * BLOCK], head_columns,
                        start=True, stop=True,
                    )
            score_of.append(score_ps[:].rearrange("n i t g -> n i g t"))

        share_of = []
        for score in score_of:
            top = work.tile([BLOCK, PAIR, HEADS], F32, name="top")
            nc.vector.tensor_reduce(top[:], score, X_AXIS, ALU.max)
            share = work.tile([BLOCK, PAIR, HEADS, K], F32, name="share")
            nc.vector.tensor_tensor(
                share[:], score, top[:].unsqueeze(3).to_broadcast([BLOCK, PAIR, HEADS, K]), ALU.subtract
            )
            nc.scalar.activation(share[:], share[:], ACT.Exp, scale=1.0 / math.sqrt(DH))
            rden = work.tile([BLOCK, PAIR, HEADS], F32, name="rden")
            nc.vector.tensor_reduce(rden[:], share[:], X_AXIS, ALU.add)
            nc.vector.reciprocal(rden[:], rden[:])
            nc.vector.tensor_tensor(
                share[:], share[:], rden[:].unsqueeze(3).to_broadcast([BLOCK, PAIR, HEADS, K]), ALU.mult
            )
            share_of.append(share)

        def weighted_values(b, first, t_inside):
            turned_ps = turned_banks.tile([BLOCK, PER_BANK, C], F32, name="turned_ps")
            for t in range(PER_BANK):
                nc.tensor.transpose(turned_ps[:, t, :], val[:, b, first + t, :], identity[:])
            turned = turned_ps[:].rearrange("n t (g d) -> n t g d", d=DH)
            share = share_of[b // PAIR][:, b % PAIR, :, first : first + PER_BANK]
            if t_inside:
                weighted = terms.tile([BLOCK, C, PER_BANK], F32, name="weighted", tag="weighted%d" % first)
                nc.vector.tensor_tensor(
                    weighted[:].rearrange("n (g d) t -> n g d t", d=DH),
                    turned.rearrange("n t g d -> n g d t"),
                    share.unsqueeze(2).to_broadcast([BLOCK, HEADS, DH, PER_BANK]),
                    ALU.mult,
                )
            else:
                weighted = terms.tile([BLOCK, PER_BANK, C], F32, name="weighted", tag="weighted%d" % first)
                nc.vector.tensor_tensor(
                    weighted[:].rearrange("n t (g d) -> n t g d", d=DH),
                    turned,
                    share.rearrange("n g t -> n t g").unsqueeze(3).to_broadcast([BLOCK, PER_BANK, HEADS, DH]),
                    ALU.mult,
                )
            return weighted

        def terms_of_block(b):
            if b in HELPED:
                products = [weighted_values(b, first, False) for first in range(0, K, PER_BANK)]
                four = terms.tile([BLOCK, PER_BANK, C], F32, name="four")
                nc.gpsimd.tensor_tensor(four[:], products[0][:], products[1][:], ALU.add)
                two = terms.tile([BLOCK, 2, C], F32, name="two")
                nc.gpsimd.tensor_tensor(two[:], four[:, 0:2, :], four[:, 2:4, :], ALU.add)
                return [two[:, 0, :], two[:, 1, :]]
            left = []
            for first in range(0, K, PER_BANK):
                if (b, first) == UNSUMMED:
                    weighted = weighted_values(b, first, False)
                    left += [weighted[:, t, :] for t in range(PER_BANK)]
                else:
                    weighted = weighted_values(b, first, True)
                    part = terms.tile([BLOCK, C], F32, name="part", tag="part%d" % first)
                    nc.vector.tensor_reduce(part[:], weighted[:], X_AXIS, ALU.add)
                    left.append(part[:])
            return left

        def mean_of_block(b, last_terms):
            columns = slice(b * BLOCK, (b + 1) * BLOCK)
            for i, term in enumerate(last_terms):
                nc.tensor.matmul(out_ps[:, columns], term, identity[:], start=(i == 0), stop=False)
            nc.tensor.matmul(out_ps[:, columns], wqr_sb[:, C : 2 * C], h[:, columns], start=False, stop=True)

        terms_of = []
        for b in range(BLOCKS + 1):
            if b < BLOCKS:
                for p in range(max(EARLY, b * PER_BLOCK), (b + 1) * PER_BLOCK):
                    values_of_piece(p)
            if b > 0:
                terms_of.append(terms_of_block(b - 1))
        out_ps = banks.tile([C, S], F32, name="out_ps", tag="bank")
        for b in (0, 2, 1, 3):
            mean_of_block(b, terms_of[b])

        for columns in (slice(0, S - BLOCK), slice(S - BLOCK, S)):
            nc.scalar.activation(result[:, columns], out_ps[:, columns], ACT.Gelu, bias=bias_res)
            nc.sync.dma_start(out[:, columns], result[:, columns])
